import numpy as np
import ml_dtypes


def mxq(x, axis, fmt="e4m3"):
    dtype, down = {"e4m3": (ml_dtypes.float8_e4m3fn, 7), "e5m2": (ml_dtypes.float8_e5m2, 14)}[fmt]
    v = np.moveaxis(np.asarray(x, np.float32).astype(ml_dtypes.bfloat16).astype(np.float64), axis, -1)
    blocks = v.reshape(v.shape[:-1] + (-1, 32))
    amax = np.abs(blocks).max(-1, keepdims=True)
    byte = np.maximum(np.where(amax > 0, np.frexp(amax)[1] - 1 + 127, 0) - down, 1)
    scale = np.exp2(byte - 127.0)
    codes = (blocks / scale).astype(np.float32).astype(dtype).astype(np.float64)
    return np.moveaxis((codes * scale).reshape(v.shape), -1, axis)


WIDE = False


def mx_kscale(k):
    if not WIDE:
        return np.ones(k)
    levels = np.array([10, -10, 5, -5, 0])
    a = np.random.permutation(np.resize(levels, k // 512 * 4)).reshape(k // 512, 4)
    idx = np.arange(k)
    return np.exp2(a[idx // 512, idx % 128 // 32])


BF16 = ml_dtypes.bfloat16


def bf(x):
    return np.asarray(x, np.float32).astype(BF16)


def f64(x):
    return np.asarray(x).astype(np.float64)


E2M1 = np.array([0.0, 0.5, 1.0, 1.5, 2.0, 3.0, 4.0, 6.0, -0.0, -0.5, -1.0, -1.5, -2.0, -3.0, -4.0, -6.0])


def pack_weight(w, fmt):
    k, n = w.shape
    w = f64(bf(w)).reshape(k // 32, 32, n)
    amax = np.abs(w).max(1)
    if fmt == "e4m3":
        byte = np.frexp(amax)[1] - 1 + 127 - 7
    else:
        mant, ex = np.frexp(amax / 6.0)
        byte = np.where(mant > 0.5, ex, ex - 1) + 127
    byte = np.clip(np.where(amax > 0, byte, 1), 1, 254)
    scaled = (w * np.exp2(127.0 - byte)[:, None, :]).reshape(k, n).astype(np.float32)
    by_word = np.ascontiguousarray(scaled.reshape(k // 512, 128, 4, n).transpose(0, 1, 3, 2))
    if fmt == "e4m3":
        words = by_word.astype(ml_dtypes.float8_e4m3fn).view(np.uint8)
    else:
        c = by_word.astype(ml_dtypes.float4_e2m1fn).view(np.uint8) & 0xF
        words = c[..., 0::2] | (c[..., 1::2] << 4)
    return np.ascontiguousarray(words), np.ascontiguousarray(byte.astype(np.uint8).reshape(k // 512, 16, n))


def unpack_weight(words, scales, fmt):
    g, p, n, _ = words.shape
    if fmt == "e4m3":
        vals = np.ascontiguousarray(words).view(ml_dtypes.float8_e4m3fn).astype(np.float64)
    else:
        nib = np.empty((g, p, n, 4), np.uint8)
        nib[..., 0::2] = words & 0xF
        nib[..., 1::2] = words >> 4
        vals = E2M1[nib]
    vals = vals * np.repeat(np.exp2(scales.astype(np.float64) - 127.0), 8, axis=1)[..., None]
    return vals.transpose(0, 1, 3, 2).reshape(g * 512, n)

def pack4(w):
    words, scales = pack_weight(w, "e2m1")
    return words.reshape(words.shape[0], 128, -1), scales


def unpack4(words, scales):
    return unpack_weight(words.reshape(words.shape[0], 128, -1, 2), scales, "e2m1")


B, H, L, E, QD = 6, 1, 128, 1024, 128
EPS = 1e-5


def build_decay_mask(num_heads, max_len):
    r = f64(np.arange(max_len))
    dec = np.array([1.0 - 2.0 ** (-5 - h) for h in range(num_heads)])
    expo = r[None, :] - r[:, None]
    return np.where(r[:, None] >= r[None, :], dec[:, None, None] ** expo[None], 0.0)


def setup_inputs():
    s = mx_kscale(E)
    kv = (0.1 + 0.32 * np.random.standard_normal((B, H, L, QD))) * (0.1 + 0.32 * np.random.standard_normal((B, H, L, QD)))
    x = bf(np.random.standard_normal((B, H, L, E)) * s)
    Wq = np.random.standard_normal((QD, E)) / np.sqrt(E) / s
    Wq_words, Wq_scales = pack4(np.ascontiguousarray(Wq.T))
    return {"x": x,
            "Wq_words": Wq_words,
            "Wq_scales": Wq_scales,
            "bq": bf(0.3 + 0.3 * np.random.standard_normal(QD)),
            "kv": bf(kv),
            "decay_mask": bf(build_decay_mask(H, L))}


def reference(x, Wq_words, Wq_scales, bq, kv, decay_mask):
    b, h, l, e = x.shape
    Q = (mxq(f64(x), 3, "e4m3") @ unpack4(Wq_words, Wq_scales)) + f64(bq)
    D = f64(decay_mask)[0, :l, :l]
    y = Q * (f64(kv) @ D.T)
    mean = y.mean(axis=(2, 3), keepdims=True)
    var = ((y - mean) ** 2).mean(axis=(2, 3), keepdims=True)
    y = (y - mean) / np.sqrt(var + EPS)
    return y.reshape(b, l, -1)

@@ -1,0 +1,205 @@
+from contextlib import ExitStack
+
+import concourse.mybir as mybir
+from concourse.masks import make_identity
+
+F32 = mybir.dt.float32
+BF16 = mybir.dt.bfloat16
+I32 = mybir.dt.int32
+U32 = mybir.dt.uint32
+U8 = mybir.dt.uint8
+FP8X4 = mybir.dt.float8_e4m3fn_x4
+FP4X4 = mybir.dt.float4_e2m1fn_x4
+ALU = mybir.AluOpType
+ACT = mybir.ActivationFunctionType
+
+P = 128
+B = 6
+L = 128
+E = 1024
+QD = 128
+PACK = 4
+PASSES = E // (P * PACK)
+PAIRS = PACK // 2
+EPS = 1e-5
+COUNT = L * QD
+
+FLOPS = 2 * B * L * E * QD + 2 * B * L * QD * QD
+
+X_LOADS = ((0, 1), (1, 3), (3, 5), (5, 6))
+
+D_SLOT = B
+BIAS_SLOT = B + 1
+SLOTS = B + 2
+
+
+def tile_parallelretention_pb_s_kernel(tc, x, Wq_words, Wq_scales, bq, kv, decay_mask, out):
+    nc = tc.nc
+    with ExitStack() as ctx:
+        keep = ctx.enter_context(tc.tile_pool(name="keep", bufs=1))
+        xt_banks = ctx.enter_context(tc.psum_pool(name="xt_banks", bufs=3))
+        q_banks = ctx.enter_context(tc.psum_pool(name="q_banks", bufs=2))
+        side_banks = ctx.enter_context(tc.psum_pool(name="side_banks", bufs=3))
+
+        x_sb = keep.tile([P, B, E], BF16)
+        small = keep.tile([P, SLOTS, P], BF16)
+        small_t = keep.tile([P, BIAS_SLOT, P], BF16)
+        w_words = keep.tile([P, PASSES, 2 * QD], U8, align_bytes=64)
+        w_planes = keep.tile([P, PASSES, QD], U8, align_bytes=64)
+        grouped = keep.tile([P, B, PASSES * L * PACK], BF16, align_bytes=64)
+        x_codes = keep.tile([P, B, PASSES * L], U32, align_bytes=64)
+        x_planes = keep.tile([P, B, PASSES * L], U8, align_bytes=64)
+        g_t = keep.tile([P, B, L], F32)
+        y_t = keep.tile([P, B, L], F32)
+        squares = keep.tile([P, B, L], F32)
+        res = keep.tile([P, B, QD], F32)
+        bias = keep.tile([P, 1], F32)
+        row_sum = keep.tile([P, B], F32)
+        row_sq = keep.tile([P, B], F32)
+        neg_mean = keep.tile([P, B], F32)
+        rstd = keep.tile([P, B], F32)
+        eps = keep.tile([P, 1], F32)
+        table_warm = keep.tile([P, 1], F32)
+        ident_f32 = keep.tile([P, P], F32)
+        ident_bf16 = keep.tile([P, P], BF16)
+        neg_inv_count = keep.tile([P, P], F32)
+
+        nc.vector.memset(w_planes[:].bitcast(I32), 0)
+        nc.vector.memset(small[:, BIAS_SLOT, :], 0.0)
+        x_rows = x.rearrange("n h l e -> l (n h) e")
+
+        def load_x(piece):
+            first, end = X_LOADS[piece]
+            nc.sync.dma_start(out=x_sb[:, first:end, :], in_=x_rows[:, first:end, :])
+
+        load_x(0)
+        for quadrant in range(4):
+            nc.sync.dma_start(
+                out=w_planes[32 * quadrant : 32 * quadrant + 4, :, :].bitcast(I32),
+                in_=Wq_scales[:, 4 * quadrant : 4 * quadrant + 4, :].rearrange("g r q -> r g q").bitcast(I32),
+            )
+        nc.sync.dma_start(out=small[:, D_SLOT, :], in_=decay_mask.rearrange("h q k -> q (h k)"))
+        nc.sync.dma_start(out=small[:, 0:B, :], in_=kv.rearrange("n h l k -> l (n h) k"))
+        load_x(1)
+        nc.sync.dma_start(out=w_words[:].bitcast(I32), in_=Wq_words.rearrange("g p b -> p g b").bitcast(I32))
+        nc.sync.dma_start(out=small[0:1, BIAS_SLOT, :], in_=bq.rearrange("(o q) -> o q", o=1))
+        load_x(2)
+        load_x(3)
+
+        nc.vector.memset(ident_f32[:], 0.0)
+        make_identity(nc, ident_f32[:], nomemset=True)
+        nc.vector.tensor_copy(out=ident_bf16[:], in_=ident_f32[:])
+        nc.vector.memset(neg_inv_count[:], -1.0 / COUNT)
+        nc.vector.memset(eps[:], EPS)
+        nc.scalar.activation(out=table_warm[:], in_=eps[:], func=ACT.Abs_reciprocal_sqrt)
+
+        def transpose_x(n):
+            x_words = x_sb[:, n, :].bitcast(F32)
+            words_per_pass = P * PAIRS
+            xt = xt_banks.tile([P, PASSES, PAIRS, L], F32)
+            for g in range(PASSES):
+                for u in range(PAIRS):
+                    nc.tensor.transpose(
+                        xt[:, g, u, :],
+                        x_words[:, words_per_pass * g + u : words_per_pass * (g + 1) : PAIRS],
+                        ident_f32[:],
+                    )
+            nc.scalar.copy(
+                out=grouped[:, n, :].bitcast(F32).rearrange("p (g l u) -> p g l u", g=PASSES, u=PAIRS),
+                in_=xt[:].rearrange("p g u l -> p g l u"),
+            )
+
+        def project(n):
+            nc.vector.quantize_mx(
+                out=x_codes[:, n, :].bitcast(FP8X4), scales=x_planes[:, n, :], in_=grouped[:, n, :]
+            )
+            q_t = q_banks.tile([P, L], F32)
+            for g in range(PASSES):
+                tokens = slice(g * L, (g + 1) * L)
+                nc.tensor.matmul_mx(
+                    out=q_t[:],
+                    lhsT=w_words[:, g, :].bitcast(FP4X4),
+                    lhsT_scale=w_planes[:, g, :],
+                    rhs=x_codes[:, n, tokens].bitcast(FP8X4),
+                    rhs_scale=x_planes[:, n, tokens],
+                    start=(g == 0),
+                    stop=(g == PASSES - 1),
+                )
+            nc.vector.scalar_tensor_tensor(
+                out=y_t[:, n, :],
+                in0=q_t[:],
+                scalar=bias[:, 0:1],
+                in1=g_t[:, n, :],
+                op0=ALU.add,
+                op1=ALU.mult,
+                accum_out=row_sum[:, n : n + 1],
+            )
+
+        def centre(n):
+            post = side_banks.tile([P, QD + 2], F32, tag="side")
+            nc.tensor.transpose(post[:, 0:QD], y_t[:, n, :], ident_f32[:])
+            nc.tensor.matmul(
+                post[:, QD : QD + 1], lhsT=neg_inv_count[:], rhs=row_sum[:, n : n + 1], start=True, stop=True
+            )
+            nc.scalar.copy(out=neg_mean[:, n : n + 1], in_=post[:, QD : QD + 1])
+            nc.scalar.activation(
+                out=squares[:, n, :],
+                in_=y_t[:, n, :],
+                func=ACT.Square,
+                bias=neg_mean[:, n : n + 1],
+                scale=1.0,
+                accum_out=row_sq[:, n : n + 1],
+            )
+            return post
+
+        def normalise(n, post):
+            nc.tensor.matmul(
+                post[:, QD + 1 : QD + 2], lhsT=neg_inv_count[:], rhs=row_sq[:, n : n + 1], start=True, stop=True
+            )
+            nc.scalar.activation(
+                out=rstd[:, n : n + 1],
+                in_=post[:, QD + 1 : QD + 2],
+                func=ACT.Abs_reciprocal_sqrt,
+                bias=eps[:, 0:1],
+                scale=-1.0,
+            )
+            nc.vector.tensor_scalar(
+                out=res[:, n, :],
+                in0=post[:, 0:QD],
+                scalar1=neg_mean[:, n : n + 1],
+                scalar2=rstd[:, n : n + 1],
+                op0=ALU.add,
+                op1=ALU.mult,
+            )
+            nc.sync.dma_start(out=out[n], in_=res[:, n, :])
+
+        def decay_product():
+            turned = side_banks.tile([P, SLOTS, P], BF16, tag="side")
+            for slot in range(BIAS_SLOT):
+                nc.tensor.transpose(turned[:, slot, :], small[:, slot, :], ident_bf16[:])
+            nc.vector.tensor_copy(out=small_t[:, 0:BIAS_SLOT, :], in_=turned[:, 0:BIAS_SLOT, :])
+            for first, end in ((0, 4), (4, B)):
+                g_bank = side_banks.tile([P, end - first, L], F32, tag="side")
+                nc.tensor.matmul(
+                    g_bank[:].rearrange("q n l -> q (n l)"),
+                    lhsT=small_t[:, D_SLOT, :],
+                    rhs=small_t[:, first:end, :].rearrange("k n l -> k (n l)"),
+                    start=True,
+                    stop=True,
+                )
+                nc.vector.tensor_copy(out=g_t[:, first:end, :], in_=g_bank[:])
+            nc.tensor.transpose(turned[:, BIAS_SLOT, :], small[:, BIAS_SLOT, :], ident_bf16[:])
+            nc.vector.tensor_copy(out=bias[:], in_=turned[:, BIAS_SLOT, 0:1])
+
+        transpose_x(0)
+        decay_product()
+        posts = {}
+        for step in range(1, B + 3):
+            if 0 <= step - 3 < B:
+                normalise(step - 3, posts[step - 3])
+            if 0 <= step - 2 < B:
+                posts[step - 2] = centre(step - 2)
+            if 0 <= step - 1 < B:
+                project(step - 1)
+            if step < B:
+                transpose_x(step)

@@ -21,6 +21,8 @@ QD = 128
 PACK = 4
 PASSES = E // (P * PACK)
 PAIRS = PACK // 2
+WINDOW = 512
+STALE = WINDOW - L
 EPS = 1e-5
 COUNT = L * QD
 
@@ -47,8 +49,8 @@ def tile_parallelretention_pb_s_kernel(tc, x, Wq_words, Wq_scales, bq, kv, decay
         w_words = keep.tile([P, PASSES, 2 * QD], U8, align_bytes=64)
         w_planes = keep.tile([P, PASSES, QD], U8, align_bytes=64)
         grouped = keep.tile([P, B, PASSES * L * PACK], BF16, align_bytes=64)
-        x_codes = keep.tile([P, B, PASSES * L], U32, align_bytes=64)
-        x_planes = keep.tile([P, B, PASSES * L], U8, align_bytes=64)
+        x_codes = keep.tile([P, STALE + B * PASSES * L], U32, align_bytes=64)
+        x_planes = keep.tile([P, STALE + B * PASSES * L], U8, align_bytes=64)
         g_t = keep.tile([P, B, L], F32)
         y_t = keep.tile([P, B, L], F32)
         squares = keep.tile([P, B, L], F32)
@@ -66,6 +68,8 @@ def tile_parallelretention_pb_s_kernel(tc, x, Wq_words, Wq_scales, bq, kv, decay
 
         nc.vector.memset(w_planes[:].bitcast(I32), 0)
         nc.vector.memset(small[:, BIAS_SLOT, :], 0.0)
+        nc.vector.memset(x_codes[:, 0:STALE].bitcast(I32), 0)
+        nc.vector.memset(x_planes[:, 0:STALE].bitcast(I32), 0)
         x_rows = x.rearrange("n h l e -> l (n h) e")
 
         def load_x(piece):
@@ -110,24 +114,23 @@ def tile_parallelretention_pb_s_kernel(tc, x, Wq_words, Wq_scales, bq, kv, decay
             )
 
         def project(n):
-            nc.vector.quantize_mx(
-                out=x_codes[:, n, :].bitcast(FP8X4), scales=x_planes[:, n, :], in_=grouped[:, n, :]
-            )
-            q_t = q_banks.tile([P, L], F32)
+            own = slice(STALE + n * PASSES * L, STALE + (n + 1) * PASSES * L)
+            nc.vector.quantize_mx(out=x_codes[:, own].bitcast(FP8X4), scales=x_planes[:, own], in_=grouped[:, n, :])
+            q_t = q_banks.tile([P, WINDOW], F32)
             for g in range(PASSES):
-                tokens = slice(g * L, (g + 1) * L)
+                window = slice((n * PASSES + g) * L, (n * PASSES + g) * L + WINDOW)
                 nc.tensor.matmul_mx(
                     out=q_t[:],
                     lhsT=w_words[:, g, :].bitcast(FP4X4),
                     lhsT_scale=w_planes[:, g, :],
-                    rhs=x_codes[:, n, tokens].bitcast(FP8X4),
-                    rhs_scale=x_planes[:, n, tokens],
+                    rhs=x_codes[:, window].bitcast(FP8X4),
+                    rhs_scale=x_planes[:, window],
                     start=(g == 0),
                     stop=(g == PASSES - 1),
                 )
             nc.vector.scalar_tensor_tensor(
                 out=y_t[:, n, :],
-                in0=q_t[:],
+                in0=q_t[:, STALE:WINDOW],
                 scalar=bias[:, 0:1],
                 in1=g_t[:, n, :],
                 op0=ALU.add,

@@ -21,8 +21,6 @@ QD = 128
 PACK = 4
 PASSES = E // (P * PACK)
 PAIRS = PACK // 2
-WINDOW = 512
-STALE = WINDOW - L
 EPS = 1e-5
 COUNT = L * QD
 
@@ -49,8 +47,8 @@ def tile_parallelretention_pb_s_kernel(tc, x, Wq_words, Wq_scales, bq, kv, decay
         w_words = keep.tile([P, PASSES, 2 * QD], U8, align_bytes=64)
         w_planes = keep.tile([P, PASSES, QD], U8, align_bytes=64)
         grouped = keep.tile([P, B, PASSES * L * PACK], BF16, align_bytes=64)
-        x_codes = keep.tile([P, STALE + B * PASSES * L], U32, align_bytes=64)
-        x_planes = keep.tile([P, STALE + B * PASSES * L], U8, align_bytes=64)
+        x_codes = keep.tile([P, B, PASSES * L], U32, align_bytes=64)
+        x_planes = keep.tile([P, B, PASSES * L], U8, align_bytes=64)
         g_t = keep.tile([P, B, L], F32)
         y_t = keep.tile([P, B, L], F32)
         squares = keep.tile([P, B, L], F32)
@@ -68,8 +66,6 @@ def tile_parallelretention_pb_s_kernel(tc, x, Wq_words, Wq_scales, bq, kv, decay
 
         nc.vector.memset(w_planes[:].bitcast(I32), 0)
         nc.vector.memset(small[:, BIAS_SLOT, :], 0.0)
-        nc.vector.memset(x_codes[:, 0:STALE].bitcast(I32), 0)
-        nc.vector.memset(x_planes[:, 0:STALE].bitcast(I32), 0)
         x_rows = x.rearrange("n h l e -> l (n h) e")
 
         def load_x(piece):
@@ -79,8 +75,8 @@ def tile_parallelretention_pb_s_kernel(tc, x, Wq_words, Wq_scales, bq, kv, decay
         load_x(0)
         for quadrant in range(4):
             nc.sync.dma_start(
-                out=w_planes[32 * quadrant : 32 * quadrant + 4, :, :].bitcast(I32),
-                in_=Wq_scales[:, 4 * quadrant : 4 * quadrant + 4, :].rearrange("g r q -> r g q").bitcast(I32),
+                out=w_planes[28 * quadrant : 28 * quadrant + 16, :, :].bitcast(I32),
+                in_=Wq_scales.rearrange("g r q -> r g q").bitcast(I32),
             )
         nc.sync.dma_start(out=small[:, D_SLOT, :], in_=decay_mask.rearrange("h q k -> q (h k)"))
         nc.sync.dma_start(out=small[:, 0:B, :], in_=kv.rearrange("n h l k -> l (n h) k"))
@@ -114,23 +110,24 @@ def tile_parallelretention_pb_s_kernel(tc, x, Wq_words, Wq_scales, bq, kv, decay
             )
 
         def project(n):
-            own = slice(STALE + n * PASSES * L, STALE + (n + 1) * PASSES * L)
-            nc.vector.quantize_mx(out=x_codes[:, own].bitcast(FP8X4), scales=x_planes[:, own], in_=grouped[:, n, :])
-            q_t = q_banks.tile([P, WINDOW], F32)
+            nc.vector.quantize_mx(
+                out=x_codes[:, n, :].bitcast(FP8X4), scales=x_planes[:, n, :], in_=grouped[:, n, :]
+            )
+            q_t = q_banks.tile([P, L], F32)
             for g in range(PASSES):
-                window = slice((n * PASSES + g) * L, (n * PASSES + g) * L + WINDOW)
+                tokens = slice(g * L, (g + 1) * L)
                 nc.tensor.matmul_mx(
                     out=q_t[:],
                     lhsT=w_words[:, g, :].bitcast(FP4X4),
                     lhsT_scale=w_planes[:, g, :],
-                    rhs=x_codes[:, window].bitcast(FP8X4),
-                    rhs_scale=x_planes[:, window],
+                    rhs=x_codes[:, n, tokens].bitcast(FP8X4),
+                    rhs_scale=x_planes[:, n, tokens],
                     start=(g == 0),
                     stop=(g == PASSES - 1),
                 )
             nc.vector.scalar_tensor_tensor(
                 out=y_t[:, n, :],
-                in0=q_t[:, STALE:WINDOW],
+                in0=q_t[:],
                 scalar=bias[:, 0:1],
                 in1=g_t[:, n, :],
                 op0=ALU.add,

@@ -26,7 +26,8 @@ COUNT = L * QD
 
 FLOPS = 2 * B * L * E * QD + 2 * B * L * QD * QD
 
-X_LOADS = ((0, 1), (1, 3), (3, 5), (5, 6))
+K_PASS = P * PACK
+X_LOADS = ((0, 1, 0, E), (1, 3, 0, E), (3, 5, 0, E), (5, 6, 0, K_PASS), (5, 6, K_PASS, E))
 
 D_SLOT = B
 BIAS_SLOT = B + 1
@@ -37,18 +38,19 @@ def tile_parallelretention_pb_s_kernel(tc, x, Wq_words, Wq_scales, bq, kv, decay
     nc = tc.nc
     with ExitStack() as ctx:
         keep = ctx.enter_context(tc.tile_pool(name="keep", bufs=1))
-        xt_banks = ctx.enter_context(tc.psum_pool(name="xt_banks", bufs=3))
+        xt_banks = ctx.enter_context(tc.psum_pool(name="xt_banks", bufs=2))
         q_banks = ctx.enter_context(tc.psum_pool(name="q_banks", bufs=2))
-        side_banks = ctx.enter_context(tc.psum_pool(name="side_banks", bufs=3))
+        y_banks = ctx.enter_context(tc.psum_pool(name="y_banks", bufs=2))
+        stat_banks = ctx.enter_context(tc.psum_pool(name="stat_banks", bufs=2))
 
         x_sb = keep.tile([P, B, E], BF16)
         small = keep.tile([P, SLOTS, P], BF16)
         small_t = keep.tile([P, BIAS_SLOT, P], BF16)
         w_words = keep.tile([P, PASSES, 2 * QD], U8, align_bytes=64)
         w_planes = keep.tile([P, PASSES, QD], U8, align_bytes=64)
-        grouped = keep.tile([P, B, PASSES * L * PACK], BF16, align_bytes=64)
-        x_codes = keep.tile([P, B, PASSES * L], U32, align_bytes=64)
-        x_planes = keep.tile([P, B, PASSES * L], U8, align_bytes=64)
+        grouped = keep.tile([P, B, PASSES, L * PACK], BF16, align_bytes=64)
+        x_codes = keep.tile([P, B, PASSES, L], U32, align_bytes=64)
+        x_planes = keep.tile([P, B, PASSES, L], U8, align_bytes=64)
         g_t = keep.tile([P, B, L], F32)
         y_t = keep.tile([P, B, L], F32)
         squares = keep.tile([P, B, L], F32)
@@ -69,8 +71,8 @@ def tile_parallelretention_pb_s_kernel(tc, x, Wq_words, Wq_scales, bq, kv, decay
         x_rows = x.rearrange("n h l e -> l (n h) e")
 
         def load_x(piece):
-            first, end = X_LOADS[piece]
-            nc.sync.dma_start(out=x_sb[:, first:end, :], in_=x_rows[:, first:end, :])
+            first, end, k_first, k_end = X_LOADS[piece]
+            nc.sync.dma_start(out=x_sb[:, first:end, k_first:k_end], in_=x_rows[:, first:end, k_first:k_end])
 
         load_x(0)
         for quadrant in range(4):
@@ -85,6 +87,7 @@ def tile_parallelretention_pb_s_kernel(tc, x, Wq_words, Wq_scales, bq, kv, decay
         nc.sync.dma_start(out=small[0:1, BIAS_SLOT, :], in_=bq.rearrange("(o q) -> o q", o=1))
         load_x(2)
         load_x(3)
+        load_x(4)
 
         nc.vector.memset(ident_f32[:], 0.0)
         make_identity(nc, ident_f32[:], nomemset=True)
@@ -96,32 +99,31 @@ def tile_parallelretention_pb_s_kernel(tc, x, Wq_words, Wq_scales, bq, kv, decay
         def transpose_x(n):
             x_words = x_sb[:, n, :].bitcast(F32)
             words_per_pass = P * PAIRS
-            xt = xt_banks.tile([P, PASSES, PAIRS, L], F32)
             for g in range(PASSES):
+                xt = xt_banks.tile([P, PAIRS, L], F32)
                 for u in range(PAIRS):
                     nc.tensor.transpose(
-                        xt[:, g, u, :],
+                        xt[:, u, :],
                         x_words[:, words_per_pass * g + u : words_per_pass * (g + 1) : PAIRS],
                         ident_f32[:],
                     )
-            nc.scalar.copy(
-                out=grouped[:, n, :].bitcast(F32).rearrange("p (g l u) -> p g l u", g=PASSES, u=PAIRS),
-                in_=xt[:].rearrange("p g u l -> p g l u"),
-            )
+                nc.scalar.copy(
+                    out=grouped[:, n, g, :].bitcast(F32).rearrange("p (l u) -> p l u", u=PAIRS),
+                    in_=xt[:].rearrange("p u l -> p l u"),
+                )
 
         def project(n):
-            nc.vector.quantize_mx(
-                out=x_codes[:, n, :].bitcast(FP8X4), scales=x_planes[:, n, :], in_=grouped[:, n, :]
-            )
             q_t = q_banks.tile([P, L], F32)
             for g in range(PASSES):
-                tokens = slice(g * L, (g + 1) * L)
+                nc.vector.quantize_mx(
+                    out=x_codes[:, n, g, :].bitcast(FP8X4), scales=x_planes[:, n, g, :], in_=grouped[:, n, g, :]
+                )
                 nc.tensor.matmul_mx(
                     out=q_t[:],
                     lhsT=w_words[:, g, :].bitcast(FP4X4),
                     lhsT_scale=w_planes[:, g, :],
-                    rhs=x_codes[:, n, tokens].bitcast(FP8X4),
-                    rhs_scale=x_planes[:, n, tokens],
+                    rhs=x_codes[:, n, g, :].bitcast(FP8X4),
+                    rhs_scale=x_planes[:, n, g, :],
                     start=(g == 0),
                     stop=(g == PASSES - 1),
                 )
@@ -136,12 +138,11 @@ def tile_parallelretention_pb_s_kernel(tc, x, Wq_words, Wq_scales, bq, kv, decay
             )
 
         def centre(n):
-            post = side_banks.tile([P, QD + 2], F32, tag="side")
-            nc.tensor.transpose(post[:, 0:QD], y_t[:, n, :], ident_f32[:])
-            nc.tensor.matmul(
-                post[:, QD : QD + 1], lhsT=neg_inv_count[:], rhs=row_sum[:, n : n + 1], start=True, stop=True
-            )
-            nc.scalar.copy(out=neg_mean[:, n : n + 1], in_=post[:, QD : QD + 1])
+            stats = stat_banks.tile([P, 2], F32, tag="stat")
+            nc.tensor.matmul(stats[:, 0:1], lhsT=neg_inv_count[:], rhs=row_sum[:, n : n + 1], start=True, stop=True)
+            y_back = y_banks.tile([P, QD], F32, tag="y")
+            nc.tensor.transpose(y_back[:], y_t[:, n, :], ident_f32[:])
+            nc.scalar.copy(out=neg_mean[:, n : n + 1], in_=stats[:, 0:1])
             nc.scalar.activation(
                 out=squares[:, n, :],
                 in_=y_t[:, n, :],
@@ -150,22 +151,20 @@ def tile_parallelretention_pb_s_kernel(tc, x, Wq_words, Wq_scales, bq, kv, decay
                 scale=1.0,
                 accum_out=row_sq[:, n : n + 1],
             )
-            return post
+            return stats, y_back
 
-        def normalise(n, post):
-            nc.tensor.matmul(
-                post[:, QD + 1 : QD + 2], lhsT=neg_inv_count[:], rhs=row_sq[:, n : n + 1], start=True, stop=True
-            )
+        def normalise(n, stats, y_back):
+            nc.tensor.matmul(stats[:, 1:2], lhsT=neg_inv_count[:], rhs=row_sq[:, n : n + 1], start=True, stop=True)
             nc.scalar.activation(
                 out=rstd[:, n : n + 1],
-                in_=post[:, QD + 1 : QD + 2],
+                in_=stats[:, 1:2],
                 func=ACT.Abs_reciprocal_sqrt,
                 bias=eps[:, 0:1],
                 scale=-1.0,
             )
             nc.vector.tensor_scalar(
                 out=res[:, n, :],
-                in0=post[:, 0:QD],
+                in0=y_back[:],
                 scalar1=neg_mean[:, n : n + 1],
                 scalar2=rstd[:, n : n + 1],
                 op0=ALU.add,
@@ -174,12 +173,12 @@ def tile_parallelretention_pb_s_kernel(tc, x, Wq_words, Wq_scales, bq, kv, decay
             nc.sync.dma_start(out=out[n], in_=res[:, n, :])
 
         def decay_product():
-            turned = side_banks.tile([P, SLOTS, P], BF16, tag="side")
+            turned = y_banks.tile([P, BIAS_SLOT, P], BF16, tag="y")
             for slot in range(BIAS_SLOT):
                 nc.tensor.transpose(turned[:, slot, :], small[:, slot, :], ident_bf16[:])
-            nc.vector.tensor_copy(out=small_t[:, 0:BIAS_SLOT, :], in_=turned[:, 0:BIAS_SLOT, :])
+            nc.vector.tensor_copy(out=small_t[:], in_=turned[:])
             for first, end in ((0, 4), (4, B)):
-                g_bank = side_banks.tile([P, end - first, L], F32, tag="side")
+                g_bank = y_banks.tile([P, end - first, L], F32, tag="y")
                 nc.tensor.matmul(
                     g_bank[:].rearrange("q n l -> q (n l)"),
                     lhsT=small_t[:, D_SLOT, :],
@@ -188,15 +187,16 @@ def tile_parallelretention_pb_s_kernel(tc, x, Wq_words, Wq_scales, bq, kv, decay
                     stop=True,
                 )
                 nc.vector.tensor_copy(out=g_t[:, first:end, :], in_=g_bank[:])
-            nc.tensor.transpose(turned[:, BIAS_SLOT, :], small[:, BIAS_SLOT, :], ident_bf16[:])
-            nc.vector.tensor_copy(out=bias[:], in_=turned[:, BIAS_SLOT, 0:1])
+            bias_turned = stat_banks.tile([P, P], BF16, tag="stat")
+            nc.tensor.transpose(bias_turned[:], small[:, BIAS_SLOT, :], ident_bf16[:])
+            nc.vector.tensor_copy(out=bias[:], in_=bias_turned[:, 0:1])
 
         transpose_x(0)
         decay_product()
         posts = {}
         for step in range(1, B + 3):
             if 0 <= step - 3 < B:
-                normalise(step - 3, posts[step - 3])
+                normalise(step - 3, *posts[step - 3])
             if 0 <= step - 2 < B:
                 posts[step - 2] = centre(step - 2)
             if 0 <= step - 1 < B:

@@ -26,8 +26,8 @@ COUNT = L * QD
 
 FLOPS = 2 * B * L * E * QD + 2 * B * L * QD * QD
 
-K_PASS = P * PACK
-X_LOADS = ((0, 1, 0, E), (1, 3, 0, E), (3, 5, 0, E), (5, 6, 0, K_PASS), (5, 6, K_PASS, E))
+GROUPS = ((0, 1), (1, 3), (3, 5), (5, 6))
+WIDEST = 2
 
 D_SLOT = B
 BIAS_SLOT = B + 1
@@ -38,19 +38,18 @@ def tile_parallelretention_pb_s_kernel(tc, x, Wq_words, Wq_scales, bq, kv, decay
     nc = tc.nc
     with ExitStack() as ctx:
         keep = ctx.enter_context(tc.tile_pool(name="keep", bufs=1))
-        xt_banks = ctx.enter_context(tc.psum_pool(name="xt_banks", bufs=2))
+        xt_banks = ctx.enter_context(tc.psum_pool(name="xt_banks", bufs=3))
         q_banks = ctx.enter_context(tc.psum_pool(name="q_banks", bufs=2))
-        y_banks = ctx.enter_context(tc.psum_pool(name="y_banks", bufs=2))
-        stat_banks = ctx.enter_context(tc.psum_pool(name="stat_banks", bufs=2))
+        side_banks = ctx.enter_context(tc.psum_pool(name="side_banks", bufs=3))
 
         x_sb = keep.tile([P, B, E], BF16)
         small = keep.tile([P, SLOTS, P], BF16)
         small_t = keep.tile([P, BIAS_SLOT, P], BF16)
         w_words = keep.tile([P, PASSES, 2 * QD], U8, align_bytes=64)
         w_planes = keep.tile([P, PASSES, QD], U8, align_bytes=64)
-        grouped = keep.tile([P, B, PASSES, L * PACK], BF16, align_bytes=64)
-        x_codes = keep.tile([P, B, PASSES, L], U32, align_bytes=64)
-        x_planes = keep.tile([P, B, PASSES, L], U8, align_bytes=64)
+        grouped = keep.tile([P, B, PASSES * L * PACK], BF16, align_bytes=64)
+        x_codes = keep.tile([P, B, PASSES * L], U32, align_bytes=64)
+        x_planes = keep.tile([P, B, PASSES * L], U8, align_bytes=64)
         g_t = keep.tile([P, B, L], F32)
         y_t = keep.tile([P, B, L], F32)
         squares = keep.tile([P, B, L], F32)
@@ -71,8 +70,8 @@ def tile_parallelretention_pb_s_kernel(tc, x, Wq_words, Wq_scales, bq, kv, decay
         x_rows = x.rearrange("n h l e -> l (n h) e")
 
         def load_x(piece):
-            first, end, k_first, k_end = X_LOADS[piece]
-            nc.sync.dma_start(out=x_sb[:, first:end, k_first:k_end], in_=x_rows[:, first:end, k_first:k_end])
+            first, end = GROUPS[piece]
+            nc.sync.dma_start(out=x_sb[:, first:end, :], in_=x_rows[:, first:end, :])
 
         load_x(0)
         for quadrant in range(4):
@@ -87,7 +86,6 @@ def tile_parallelretention_pb_s_kernel(tc, x, Wq_words, Wq_scales, bq, kv, decay
         nc.sync.dma_start(out=small[0:1, BIAS_SLOT, :], in_=bq.rearrange("(o q) -> o q", o=1))
         load_x(2)
         load_x(3)
-        load_x(4)
 
         nc.vector.memset(ident_f32[:], 0.0)
         make_identity(nc, ident_f32[:], nomemset=True)
@@ -99,31 +97,32 @@ def tile_parallelretention_pb_s_kernel(tc, x, Wq_words, Wq_scales, bq, kv, decay
         def transpose_x(n):
             x_words = x_sb[:, n, :].bitcast(F32)
             words_per_pass = P * PAIRS
+            xt = xt_banks.tile([P, PASSES, PAIRS, L], F32)
             for g in range(PASSES):
-                xt = xt_banks.tile([P, PAIRS, L], F32)
                 for u in range(PAIRS):
                     nc.tensor.transpose(
-                        xt[:, u, :],
+                        xt[:, g, u, :],
                         x_words[:, words_per_pass * g + u : words_per_pass * (g + 1) : PAIRS],
                         ident_f32[:],
                     )
-                nc.scalar.copy(
-                    out=grouped[:, n, g, :].bitcast(F32).rearrange("p (l u) -> p l u", u=PAIRS),
-                    in_=xt[:].rearrange("p u l -> p l u"),
-                )
+            nc.scalar.copy(
+                out=grouped[:, n, :].bitcast(F32).rearrange("p (g l u) -> p g l u", g=PASSES, u=PAIRS),
+                in_=xt[:].rearrange("p g u l -> p g l u"),
+            )
 
         def project(n):
+            nc.vector.quantize_mx(
+                out=x_codes[:, n, :].bitcast(FP8X4), scales=x_planes[:, n, :], in_=grouped[:, n, :]
+            )
             q_t = q_banks.tile([P, L], F32)
             for g in range(PASSES):
-                nc.vector.quantize_mx(
-                    out=x_codes[:, n, g, :].bitcast(FP8X4), scales=x_planes[:, n, g, :], in_=grouped[:, n, g, :]
-                )
+                tokens = slice(g * L, (g + 1) * L)
                 nc.tensor.matmul_mx(
                     out=q_t[:],
                     lhsT=w_words[:, g, :].bitcast(FP4X4),
                     lhsT_scale=w_planes[:, g, :],
-                    rhs=x_codes[:, n, g, :].bitcast(FP8X4),
-                    rhs_scale=x_planes[:, n, g, :],
+                    rhs=x_codes[:, n, tokens].bitcast(FP8X4),
+                    rhs_scale=x_planes[:, n, tokens],
                     start=(g == 0),
                     stop=(g == PASSES - 1),
                 )
@@ -137,48 +136,65 @@ def tile_parallelretention_pb_s_kernel(tc, x, Wq_words, Wq_scales, bq, kv, decay
                 accum_out=row_sum[:, n : n + 1],
             )
 
-        def centre(n):
-            stats = stat_banks.tile([P, 2], F32, tag="stat")
-            nc.tensor.matmul(stats[:, 0:1], lhsT=neg_inv_count[:], rhs=row_sum[:, n : n + 1], start=True, stop=True)
-            y_back = y_banks.tile([P, QD], F32, tag="y")
-            nc.tensor.transpose(y_back[:], y_t[:, n, :], ident_f32[:])
-            nc.scalar.copy(out=neg_mean[:, n : n + 1], in_=stats[:, 0:1])
-            nc.scalar.activation(
-                out=squares[:, n, :],
-                in_=y_t[:, n, :],
-                func=ACT.Square,
-                bias=neg_mean[:, n : n + 1],
-                scale=1.0,
-                accum_out=row_sq[:, n : n + 1],
-            )
-            return stats, y_back
+        MEANS = WIDEST * QD
+        VARS = MEANS + WIDEST
 
-        def normalise(n, stats, y_back):
-            nc.tensor.matmul(stats[:, 1:2], lhsT=neg_inv_count[:], rhs=row_sq[:, n : n + 1], start=True, stop=True)
+        def centre(first, end):
+            post = side_banks.tile([P, VARS + WIDEST], F32, tag="side")
+            for n in range(first, end):
+                nc.tensor.transpose(post[:, (n - first) * QD : (n - first + 1) * QD], y_t[:, n, :], ident_f32[:])
+            nc.tensor.matmul(
+                post[:, MEANS : MEANS + end - first],
+                lhsT=neg_inv_count[:],
+                rhs=row_sum[:, first:end],
+                start=True,
+                stop=True,
+            )
+            nc.scalar.copy(out=neg_mean[:, first:end], in_=post[:, MEANS : MEANS + end - first])
+            for n in range(first, end):
+                nc.scalar.activation(
+                    out=squares[:, n, :],
+                    in_=y_t[:, n, :],
+                    func=ACT.Square,
+                    bias=neg_mean[:, n : n + 1],
+                    scale=1.0,
+                    accum_out=row_sq[:, n : n + 1],
+                )
+            return post
+
+        def normalise(first, end, post):
+            nc.tensor.matmul(
+                post[:, VARS : VARS + end - first],
+                lhsT=neg_inv_count[:],
+                rhs=row_sq[:, first:end],
+                start=True,
+                stop=True,
+            )
             nc.scalar.activation(
-                out=rstd[:, n : n + 1],
-                in_=stats[:, 1:2],
+                out=rstd[:, first:end],
+                in_=post[:, VARS : VARS + end - first],
                 func=ACT.Abs_reciprocal_sqrt,
                 bias=eps[:, 0:1],
                 scale=-1.0,
             )
-            nc.vector.tensor_scalar(
-                out=res[:, n, :],
-                in0=y_back[:],
-                scalar1=neg_mean[:, n : n + 1],
-                scalar2=rstd[:, n : n + 1],
-                op0=ALU.add,
-                op1=ALU.mult,
-            )
-            nc.sync.dma_start(out=out[n], in_=res[:, n, :])
+            for n in range(first, end):
+                nc.vector.tensor_scalar(
+                    out=res[:, n, :],
+                    in0=post[:, (n - first) * QD : (n - first + 1) * QD],
+                    scalar1=neg_mean[:, n : n + 1],
+                    scalar2=rstd[:, n : n + 1],
+                    op0=ALU.add,
+                    op1=ALU.mult,
+                )
+            nc.sync.dma_start(out=out[first:end].rearrange("n l q -> l n q"), in_=res[:, first:end, :])
 
         def decay_product():
-            turned = y_banks.tile([P, BIAS_SLOT, P], BF16, tag="y")
+            turned = side_banks.tile([P, SLOTS, P], BF16, tag="side")
             for slot in range(BIAS_SLOT):
                 nc.tensor.transpose(turned[:, slot, :], small[:, slot, :], ident_bf16[:])
-            nc.vector.tensor_copy(out=small_t[:], in_=turned[:])
+            nc.vector.tensor_copy(out=small_t[:, 0:BIAS_SLOT, :], in_=turned[:, 0:BIAS_SLOT, :])
             for first, end in ((0, 4), (4, B)):
-                g_bank = y_banks.tile([P, end - first, L], F32, tag="y")
+                g_bank = side_banks.tile([P, end - first, L], F32, tag="side")
                 nc.tensor.matmul(
                     g_bank[:].rearrange("q n l -> q (n l)"),
                     lhsT=small_t[:, D_SLOT, :],
@@ -187,19 +203,15 @@ def tile_parallelretention_pb_s_kernel(tc, x, Wq_words, Wq_scales, bq, kv, decay
                     stop=True,
                 )
                 nc.vector.tensor_copy(out=g_t[:, first:end, :], in_=g_bank[:])
-            bias_turned = stat_banks.tile([P, P], BF16, tag="stat")
-            nc.tensor.transpose(bias_turned[:], small[:, BIAS_SLOT, :], ident_bf16[:])
-            nc.vector.tensor_copy(out=bias[:], in_=bias_turned[:, 0:1])
+            nc.tensor.transpose(turned[:, BIAS_SLOT, :], small[:, BIAS_SLOT, :], ident_bf16[:])
+            nc.vector.tensor_copy(out=bias[:], in_=turned[:, BIAS_SLOT, 0:1])
 
         transpose_x(0)
         decay_product()
-        posts = {}
-        for step in range(1, B + 3):
-            if 0 <= step - 3 < B:
-                normalise(step - 3, *posts[step - 3])
-            if 0 <= step - 2 < B:
-                posts[step - 2] = centre(step - 2)
-            if 0 <= step - 1 < B:
-                project(step - 1)
-            if step < B:
-                transpose_x(step)
+        for first, end in GROUPS:
+            for n in range(max(first, 1), end):
+                transpose_x(n)
+            for n in range(first, end):
+                project(n)
+            post = centre(first, end)
+            normalise(first, end, post)

@@ -85,7 +85,9 @@ def tile_parallelretention_pb_s_kernel(tc, x, Wq_words, Wq_scales, bq, kv, decay
         nc.sync.dma_start(out=w_words[:].bitcast(I32), in_=Wq_words.rearrange("g p b -> p g b").bitcast(I32))
         nc.sync.dma_start(out=small[0:1, BIAS_SLOT, :], in_=bq.rearrange("(o q) -> o q", o=1))
         load_x(2)
-        load_x(3)
+        for g in range(PASSES):
+            half = slice(g * P * PACK, (g + 1) * P * PACK)
+            nc.sync.dma_start(out=x_sb[:, B - 1, half], in_=x_rows[:, B - 1, half])
 
         nc.vector.memset(ident_f32[:], 0.0)
         make_identity(nc, ident_f32[:], nomemset=True)
@@ -111,9 +113,10 @@ def tile_parallelretention_pb_s_kernel(tc, x, Wq_words, Wq_scales, bq, kv, decay
             )
 
         def project(n):
-            nc.vector.quantize_mx(
-                out=x_codes[:, n, :].bitcast(FP8X4), scales=x_planes[:, n, :], in_=grouped[:, n, :]
-            )
+            if n < B - 1:
+                nc.vector.quantize_mx(
+                    out=x_codes[:, n, :].bitcast(FP8X4), scales=x_planes[:, n, :], in_=grouped[:, n, :]
+                )
             q_t = q_banks.tile([P, L], F32)
             for g in range(PASSES):
                 tokens = slice(g * L, (g + 1) * L)
@@ -134,6 +137,26 @@ def tile_parallelretention_pb_s_kernel(tc, x, Wq_words, Wq_scales, bq, kv, decay
                 op0=ALU.add,
                 op1=ALU.mult,
                 accum_out=row_sum[:, n : n + 1],
+            )
+
+        def transpose_half(n, g):
+            x_words = x_sb[:, n, :].bitcast(F32)
+            words_per_pass = P * PAIRS
+            xt = xt_banks.tile([P, PAIRS, L], F32, name="xt")
+            for u in range(PAIRS):
+                nc.tensor.transpose(
+                    xt[:, u, :],
+                    x_words[:, words_per_pass * g + u : words_per_pass * (g + 1) : PAIRS],
+                    ident_f32[:],
+                )
+            values = slice(g * L * PACK, (g + 1) * L * PACK)
+            tokens = slice(g * L, (g + 1) * L)
+            nc.scalar.copy(
+                out=grouped[:, n, values].bitcast(F32).rearrange("p (l u) -> p l u", u=PAIRS),
+                in_=xt[:].rearrange("p u l -> p l u"),
+            )
+            nc.vector.quantize_mx(
+                out=x_codes[:, n, tokens].bitcast(FP8X4), scales=x_planes[:, n, tokens], in_=grouped[:, n, values]
             )
 
         MEANS = WIDEST * QD
@@ -210,7 +233,11 @@ def tile_parallelretention_pb_s_kernel(tc, x, Wq_words, Wq_scales, bq, kv, decay
         decay_product()
         for first, end in GROUPS:
             for n in range(max(first, 1), end):
-                transpose_x(n)
+                if n < B - 1:
+                    transpose_x(n)
+                else:
+                    for g in range(PASSES):
+                        transpose_half(n, g)
             for n in range(first, end):
                 project(n)
             post = centre(first, end)

@@ -229,16 +229,32 @@ def tile_parallelretention_pb_s_kernel(tc, x, Wq_words, Wq_scales, bq, kv, decay
             nc.tensor.transpose(turned[:, BIAS_SLOT, :], small[:, BIAS_SLOT, :], ident_bf16[:])
             nc.vector.tensor_copy(out=bias[:], in_=turned[:, BIAS_SLOT, 0:1])
 
-        transpose_x(0)
-        decay_product()
-        for first, end in GROUPS:
-            for n in range(max(first, 1), end):
+        def turn_group(first, end):
+            for n in range(first, end):
                 if n < B - 1:
                     transpose_x(n)
                 else:
                     for g in range(PASSES):
                         transpose_half(n, g)
+
+        def project_group(first, end):
             for n in range(first, end):
                 project(n)
-            post = centre(first, end)
-            normalise(first, end, post)
+
+        turn_group(*GROUPS[0])
+        decay_product()
+        turn_group(*GROUPS[1])
+        project_group(*GROUPS[0])
+        turn_group(*GROUPS[2])
+        project_group(*GROUPS[1])
+        post_0 = centre(*GROUPS[0])
+        normalise(*GROUPS[0], post_0)
+        turn_group(*GROUPS[3])
+        project_group(*GROUPS[2])
+        post_1 = centre(*GROUPS[1])
+        normalise(*GROUPS[1], post_1)
+        project_group(*GROUPS[3])
+        post_2 = centre(*GROUPS[2])
+        post_3 = centre(*GROUPS[3])
+        normalise(*GROUPS[2], post_2)
+        normalise(*GROUPS[3], post_3)

@@ -27,7 +27,8 @@ COUNT = L * QD
 FLOPS = 2 * B * L * E * QD + 2 * B * L * QD * QD
 
 GROUPS = ((0, 1), (1, 3), (3, 5), (5, 6))
-WIDEST = 2
+WIDEST = 3
+SHARED = ((0, 3), (3, 5), (5, 6))
 
 D_SLOT = B
 BIAS_SLOT = B + 1
@@ -247,14 +248,12 @@ def tile_parallelretention_pb_s_kernel(tc, x, Wq_words, Wq_scales, bq, kv, decay
         project_group(*GROUPS[0])
         turn_group(*GROUPS[2])
         project_group(*GROUPS[1])
-        post_0 = centre(*GROUPS[0])
-        normalise(*GROUPS[0], post_0)
         turn_group(*GROUPS[3])
+        post_0 = centre(*SHARED[0])
+        normalise(*SHARED[0], post_0)
         project_group(*GROUPS[2])
-        post_1 = centre(*GROUPS[1])
-        normalise(*GROUPS[1], post_1)
         project_group(*GROUPS[3])
-        post_2 = centre(*GROUPS[2])
-        post_3 = centre(*GROUPS[3])
-        normalise(*GROUPS[2], post_2)
-        normalise(*GROUPS[3], post_3)
+        post_1 = centre(*SHARED[1])
+        post_2 = centre(*SHARED[2])
+        normalise(*SHARED[1], post_1)
+        normalise(*SHARED[2], post_2)

@@ -23,16 +23,17 @@ PASSES = E // (P * PACK)
 PAIRS = PACK // 2
 EPS = 1e-5
 COUNT = L * QD
+LAST = B - 1
 
 FLOPS = 2 * B * L * E * QD + 2 * B * L * QD * QD
 
-GROUPS = ((0, 1), (1, 3), (3, 5), (5, 6))
+WARM = 3
 WIDEST = 3
-SHARED = ((0, 3), (3, 5), (5, 6))
 
 D_SLOT = B
 BIAS_SLOT = B + 1
 SLOTS = B + 2
+CUT = 4
 
 
 def tile_parallelretention_pb_s_kernel(tc, x, Wq_words, Wq_scales, bq, kv, decay_mask, out):
@@ -42,6 +43,7 @@ def tile_parallelretention_pb_s_kernel(tc, x, Wq_words, Wq_scales, bq, kv, decay
         xt_banks = ctx.enter_context(tc.psum_pool(name="xt_banks", bufs=3))
         q_banks = ctx.enter_context(tc.psum_pool(name="q_banks", bufs=2))
         side_banks = ctx.enter_context(tc.psum_pool(name="side_banks", bufs=3))
+        ctx.enter_context(tc.manual_schedule())
 
         x_sb = keep.tile([P, B, E], BF16)
         small = keep.tile([P, SLOTS, P], BF16)
@@ -66,59 +68,73 @@ def tile_parallelretention_pb_s_kernel(tc, x, Wq_words, Wq_scales, bq, kv, decay
         ident_bf16 = keep.tile([P, P], BF16)
         neg_inv_count = keep.tile([P, P], F32)
 
+        nc.vector.memset(neg_inv_count[:], -1.0 / COUNT)
+        nc.vector.memset(eps[:], EPS)
         nc.vector.memset(w_planes[:].bitcast(I32), 0)
+        nc.vector.memset(ident_f32[:], 0.0)
         nc.vector.memset(small[:, BIAS_SLOT, :], 0.0)
+        nc.scalar.activation(out=table_warm[:], in_=eps[:], func=ACT.Abs_reciprocal_sqrt)
+        make_identity(nc, ident_f32[:], nomemset=True)
+        nc.vector.tensor_copy(out=ident_bf16[:], in_=ident_f32[:])
+        idle = xt_banks.tile([P, WARM, P], F32, tag="xt")
+        for i in range(WARM):
+            nc.tensor.matmul(idle[:, i, :], lhsT=neg_inv_count[:], rhs=neg_inv_count[:], start=True, stop=True)
+
         x_rows = x.rearrange("n h l e -> l (n h) e")
 
-        def load_x(piece):
-            first, end = GROUPS[piece]
+        def load_x(first, end):
             nc.sync.dma_start(out=x_sb[:, first:end, :], in_=x_rows[:, first:end, :])
 
-        load_x(0)
-        for quadrant in range(4):
+        def load_scales(quadrant):
             nc.sync.dma_start(
                 out=w_planes[28 * quadrant : 28 * quadrant + 16, :, :].bitcast(I32),
                 in_=Wq_scales.rearrange("g r q -> r g q").bitcast(I32),
             )
+
+        nc.sync.dma_start(
+            out=small[:, 0:B, :], in_=kv.rearrange("n h l k -> (n h l) k").rearrange("(p j) k -> p j k", j=B)
+        )
         nc.sync.dma_start(out=small[:, D_SLOT, :], in_=decay_mask.rearrange("h q k -> q (h k)"))
-        nc.sync.dma_start(out=small[:, 0:B, :], in_=kv.rearrange("n h l k -> l (n h) k"))
-        load_x(1)
+        load_x(0, 1)
         nc.sync.dma_start(out=w_words[:].bitcast(I32), in_=Wq_words.rearrange("g p b -> p g b").bitcast(I32))
+        load_x(1, 3)
+        for quadrant in range(3):
+            load_scales(quadrant)
+        load_scales(3)
+        load_x(3, 5)
         nc.sync.dma_start(out=small[0:1, BIAS_SLOT, :], in_=bq.rearrange("(o q) -> o q", o=1))
-        load_x(2)
         for g in range(PASSES):
             half = slice(g * P * PACK, (g + 1) * P * PACK)
-            nc.sync.dma_start(out=x_sb[:, B - 1, half], in_=x_rows[:, B - 1, half])
+            nc.sync.dma_start(out=x_sb[:, LAST, half], in_=x_rows[:, LAST, half])
 
-        nc.vector.memset(ident_f32[:], 0.0)
-        make_identity(nc, ident_f32[:], nomemset=True)
-        nc.vector.tensor_copy(out=ident_bf16[:], in_=ident_f32[:])
-        nc.vector.memset(neg_inv_count[:], -1.0 / COUNT)
-        nc.vector.memset(eps[:], EPS)
-        nc.scalar.activation(out=table_warm[:], in_=eps[:], func=ACT.Abs_reciprocal_sqrt)
+        WORDS = P * PAIRS
 
-        def transpose_x(n):
+        def turn(n, passes):
+            xt = xt_banks.tile([P, len(passes), PAIRS, L], F32, name="xt")
             x_words = x_sb[:, n, :].bitcast(F32)
-            words_per_pass = P * PAIRS
-            xt = xt_banks.tile([P, PASSES, PAIRS, L], F32)
-            for g in range(PASSES):
+            for i, g in enumerate(passes):
                 for u in range(PAIRS):
                     nc.tensor.transpose(
-                        xt[:, g, u, :],
-                        x_words[:, words_per_pass * g + u : words_per_pass * (g + 1) : PAIRS],
-                        ident_f32[:],
+                        xt[:, i, u, :], x_words[:, WORDS * g + u : WORDS * (g + 1) : PAIRS], ident_f32[:]
                     )
+            return xt
+
+        def group(n, passes, xt):
+            values = slice(passes[0] * L * PACK, (passes[-1] + 1) * L * PACK)
             nc.scalar.copy(
-                out=grouped[:, n, :].bitcast(F32).rearrange("p (g l u) -> p g l u", g=PASSES, u=PAIRS),
+                out=grouped[:, n, values].bitcast(F32).rearrange("p (g l u) -> p g l u", l=L, u=PAIRS),
                 in_=xt[:].rearrange("p g u l -> p g l u"),
             )
 
+        def quantise(n, passes):
+            values = slice(passes[0] * L * PACK, (passes[-1] + 1) * L * PACK)
+            tokens = slice(passes[0] * L, (passes[-1] + 1) * L)
+            nc.vector.quantize_mx(
+                out=x_codes[:, n, tokens].bitcast(FP8X4), scales=x_planes[:, n, tokens], in_=grouped[:, n, values]
+            )
+
         def project(n):
-            if n < B - 1:
-                nc.vector.quantize_mx(
-                    out=x_codes[:, n, :].bitcast(FP8X4), scales=x_planes[:, n, :], in_=grouped[:, n, :]
-                )
-            q_t = q_banks.tile([P, L], F32)
+            q_t = q_banks.tile([P, L], F32, name="q_t")
             for g in range(PASSES):
                 tokens = slice(g * L, (g + 1) * L)
                 nc.tensor.matmul_mx(
@@ -130,6 +146,9 @@ def tile_parallelretention_pb_s_kernel(tc, x, Wq_words, Wq_scales, bq, kv, decay
                     start=(g == 0),
                     stop=(g == PASSES - 1),
                 )
+            return q_t
+
+        def multiply(n, q_t):
             nc.vector.scalar_tensor_tensor(
                 out=y_t[:, n, :],
                 in0=q_t[:],
@@ -140,41 +159,15 @@ def tile_parallelretention_pb_s_kernel(tc, x, Wq_words, Wq_scales, bq, kv, decay
                 accum_out=row_sum[:, n : n + 1],
             )
 
-        def transpose_half(n, g):
-            x_words = x_sb[:, n, :].bitcast(F32)
-            words_per_pass = P * PAIRS
-            xt = xt_banks.tile([P, PAIRS, L], F32, name="xt")
-            for u in range(PAIRS):
-                nc.tensor.transpose(
-                    xt[:, u, :],
-                    x_words[:, words_per_pass * g + u : words_per_pass * (g + 1) : PAIRS],
-                    ident_f32[:],
-                )
-            values = slice(g * L * PACK, (g + 1) * L * PACK)
-            tokens = slice(g * L, (g + 1) * L)
-            nc.scalar.copy(
-                out=grouped[:, n, values].bitcast(F32).rearrange("p (l u) -> p l u", u=PAIRS),
-                in_=xt[:].rearrange("p u l -> p l u"),
-            )
-            nc.vector.quantize_mx(
-                out=x_codes[:, n, tokens].bitcast(FP8X4), scales=x_planes[:, n, tokens], in_=grouped[:, n, values]
-            )
+        def sum_features(columns, stats):
+            nc.tensor.matmul(stats, lhsT=neg_inv_count[:], rhs=columns, start=True, stop=True)
 
-        MEANS = WIDEST * QD
-        VARS = MEANS + WIDEST
-
-        def centre(first, end):
-            post = side_banks.tile([P, VARS + WIDEST], F32, tag="side")
+        def turn_back(first, end, back):
             for n in range(first, end):
-                nc.tensor.transpose(post[:, (n - first) * QD : (n - first + 1) * QD], y_t[:, n, :], ident_f32[:])
-            nc.tensor.matmul(
-                post[:, MEANS : MEANS + end - first],
-                lhsT=neg_inv_count[:],
-                rhs=row_sum[:, first:end],
-                start=True,
-                stop=True,
-            )
-            nc.scalar.copy(out=neg_mean[:, first:end], in_=post[:, MEANS : MEANS + end - first])
+                nc.tensor.transpose(back[:, n - first, :], y_t[:, n, :], ident_f32[:])
+
+        def square(first, end, stats):
+            nc.scalar.copy(out=neg_mean[:, first:end], in_=stats)
             for n in range(first, end):
                 nc.scalar.activation(
                     out=squares[:, n, :],
@@ -184,27 +177,17 @@ def tile_parallelretention_pb_s_kernel(tc, x, Wq_words, Wq_scales, bq, kv, decay
                     scale=1.0,
                     accum_out=row_sq[:, n : n + 1],
                 )
-            return post
 
-        def normalise(first, end, post):
-            nc.tensor.matmul(
-                post[:, VARS : VARS + end - first],
-                lhsT=neg_inv_count[:],
-                rhs=row_sq[:, first:end],
-                start=True,
-                stop=True,
-            )
+        def deviation(first, end, stats):
             nc.scalar.activation(
-                out=rstd[:, first:end],
-                in_=post[:, VARS : VARS + end - first],
-                func=ACT.Abs_reciprocal_sqrt,
-                bias=eps[:, 0:1],
-                scale=-1.0,
+                out=rstd[:, first:end], in_=stats, func=ACT.Abs_reciprocal_sqrt, bias=eps[:, 0:1], scale=-1.0
             )
+
+        def normalise(first, end, back):
             for n in range(first, end):
                 nc.vector.tensor_scalar(
                     out=res[:, n, :],
-                    in0=post[:, (n - first) * QD : (n - first + 1) * QD],
+                    in0=back[:, n - first, :],
                     scalar1=neg_mean[:, n : n + 1],
                     scalar2=rstd[:, n : n + 1],
                     op0=ALU.add,
@@ -212,48 +195,89 @@ def tile_parallelretention_pb_s_kernel(tc, x, Wq_words, Wq_scales, bq, kv, decay
                 )
             nc.sync.dma_start(out=out[first:end].rearrange("n l q -> l n q"), in_=res[:, first:end, :])
 
-        def decay_product():
-            turned = side_banks.tile([P, SLOTS, P], BF16, tag="side")
-            for slot in range(BIAS_SLOT):
-                nc.tensor.transpose(turned[:, slot, :], small[:, slot, :], ident_bf16[:])
-            nc.vector.tensor_copy(out=small_t[:, 0:BIAS_SLOT, :], in_=turned[:, 0:BIAS_SLOT, :])
-            for first, end in ((0, 4), (4, B)):
-                g_bank = side_banks.tile([P, end - first, L], F32, tag="side")
-                nc.tensor.matmul(
-                    g_bank[:].rearrange("q n l -> q (n l)"),
-                    lhsT=small_t[:, D_SLOT, :],
-                    rhs=small_t[:, first:end, :].rearrange("k n l -> k (n l)"),
-                    start=True,
-                    stop=True,
-                )
-                nc.vector.tensor_copy(out=g_t[:, first:end, :], in_=g_bank[:])
-            nc.tensor.transpose(turned[:, BIAS_SLOT, :], small[:, BIAS_SLOT, :], ident_bf16[:])
-            nc.vector.tensor_copy(out=bias[:], in_=turned[:, BIAS_SLOT, 0:1])
+        BOTH = (0, 1)
 
-        def turn_group(first, end):
-            for n in range(first, end):
-                if n < B - 1:
-                    transpose_x(n)
-                else:
-                    for g in range(PASSES):
-                        transpose_half(n, g)
+        turned = side_banks.tile([P, B, P], BF16, tag="side")
+        for j in range(B):
+            nc.tensor.transpose(turned[:, j, :], small[:, j, :], ident_bf16[:])
+        nc.vector.tensor_copy(
+            out=small_t[:, 0:B, :].rearrange("k n l -> k (n l)").rearrange("k (p j) -> k p j", j=B),
+            in_=turned[:].rearrange("k j p -> k p j"),
+        )
+        turned_2 = side_banks.tile([P, 2, P], BF16, tag="side")
+        nc.tensor.transpose(turned_2[:, 0, :], small[:, D_SLOT, :], ident_bf16[:])
+        nc.scalar.copy(out=small_t[:, D_SLOT, :], in_=turned_2[:, 0, :])
+        xt_0 = turn(0, BOTH)
+        group(0, BOTH, xt_0)
+        quantise(0, BOTH)
+        xt_1 = turn(1, BOTH)
+        group(1, BOTH, xt_1)
 
-        def project_group(first, end):
-            for n in range(first, end):
-                project(n)
+        g_first = side_banks.tile([P, CUT, L], F32, tag="side")
+        g_second = side_banks.tile([P, B - CUT, L], F32, tag="side")
+        for bank, first, end in ((g_first, 0, CUT), (g_second, CUT, B)):
+            nc.tensor.matmul(
+                bank[:].rearrange("q n l -> q (n l)"),
+                lhsT=small_t[:, D_SLOT, :],
+                rhs=small_t[:, first:end, :].rearrange("k n l -> k (n l)"),
+                start=True,
+                stop=True,
+            )
+        nc.vector.tensor_copy(out=g_t[:, 0:CUT, :], in_=g_first[:])
+        xt_2 = turn(2, BOTH)
+        group(2, BOTH, xt_2)
+        nc.scalar.copy(out=g_t[:, CUT:B, :], in_=g_second[:])
+        nc.tensor.transpose(turned_2[:, 1, :], small[:, BIAS_SLOT, :], ident_bf16[:])
+        nc.vector.tensor_copy(out=bias[:], in_=turned_2[:, 1, 0:1])
 
-        turn_group(*GROUPS[0])
-        decay_product()
-        turn_group(*GROUPS[1])
-        project_group(*GROUPS[0])
-        turn_group(*GROUPS[2])
-        project_group(*GROUPS[1])
-        turn_group(*GROUPS[3])
-        post_0 = centre(*SHARED[0])
-        normalise(*SHARED[0], post_0)
-        project_group(*GROUPS[2])
-        project_group(*GROUPS[3])
-        post_1 = centre(*SHARED[1])
-        post_2 = centre(*SHARED[2])
-        normalise(*SHARED[1], post_1)
-        normalise(*SHARED[2], post_2)
+        xt_3 = turn(3, BOTH)
+        group(3, BOTH, xt_3)
+        q_0 = project(0)
+        quantise(1, BOTH)
+        multiply(0, q_0)
+        xt_4 = turn(4, BOTH)
+        group(4, BOTH, xt_4)
+        q_1 = project(1)
+        quantise(2, BOTH)
+        multiply(1, q_1)
+        xt_5a = turn(LAST, (0,))
+        group(LAST, (0,), xt_5a)
+        q_2 = project(2)
+        quantise(3, BOTH)
+        multiply(2, q_2)
+        xt_5b = turn(LAST, (1,))
+        group(LAST, (1,), xt_5b)
+        q_3 = project(3)
+        quantise(4, BOTH)
+        multiply(3, q_3)
+
+        back_0 = side_banks.tile([P, 3, QD], F32, tag="side")
+        stats_0 = side_banks.tile([P, 2, WIDEST], F32, tag="side")
+        sum_features(row_sum[:, 0:3], stats_0[:, 0, 0:3])
+        square(0, 3, stats_0[:, 0, 0:3])
+        q_4 = project(4)
+        quantise(LAST, (0,))
+        quantise(LAST, (1,))
+        multiply(4, q_4)
+        turn_back(0, 3, back_0)
+        q_5 = project(LAST)
+        multiply(LAST, q_5)
+        back_1 = side_banks.tile([P, 2, QD], F32, tag="side")
+        stats_1 = xt_banks.tile([P, 2, WIDEST], F32, tag="xt")
+        sum_features(row_sum[:, 3:5], stats_1[:, 0, 0:2])
+        square(3, 5, stats_1[:, 0, 0:2])
+        sum_features(row_sq[:, 0:3], stats_0[:, 1, 0:3])
+        deviation(0, 3, stats_0[:, 1, 0:3])
+        normalise(0, 3, back_0)
+        back_2 = xt_banks.tile([P, 1, QD], F32, tag="xt")
+        stats_2 = xt_banks.tile([P, 2, WIDEST], F32, tag="xt")
+        sum_features(row_sum[:, 5:6], stats_2[:, 0, 0:1])
+        square(5, 6, stats_2[:, 0, 0:1])
+        turn_back(3, 5, back_1)
+        turn_back(5, 6, back_2)
+        sum_features(row_sq[:, 3:5], stats_1[:, 1, 0:2])
+        deviation(3, 5, stats_1[:, 1, 0:2])
+        normalise(3, 5, back_1)
+        sum_features(row_sq[:, 5:6], stats_2[:, 1, 0:1])
+        deviation(5, 6, stats_2[:, 1, 0:1])
+        normalise(5, 6, back_2)

@@ -28,6 +28,7 @@ LAST = B - 1
 FLOPS = 2 * B * L * E * QD + 2 * B * L * QD * QD
 
 WARM = 3
+IDLE = 512
 WIDEST = 3
 
 D_SLOT = B
@@ -63,6 +64,9 @@ def tile_parallelretention_pb_s_kernel(tc, x, Wq_words, Wq_scales, bq, kv, decay
         neg_mean = keep.tile([P, B], F32)
         rstd = keep.tile([P, B], F32)
         eps = keep.tile([P, 1], F32)
+        idle_values = keep.tile([P, IDLE * PACK], BF16, align_bytes=64)
+        idle_codes = keep.tile([P, IDLE], U32, align_bytes=64)
+        idle_plane = keep.tile([P, IDLE], U8, align_bytes=64)
         table_warm = keep.tile([P, 1], F32)
         ident_f32 = keep.tile([P, P], F32)
         ident_bf16 = keep.tile([P, P], BF16)
@@ -75,10 +79,13 @@ def tile_parallelretention_pb_s_kernel(tc, x, Wq_words, Wq_scales, bq, kv, decay
         nc.vector.memset(small[:, BIAS_SLOT, :], 0.0)
         nc.scalar.activation(out=table_warm[:], in_=eps[:], func=ACT.Abs_reciprocal_sqrt)
         make_identity(nc, ident_f32[:], nomemset=True)
+        nc.vector.memset(idle_values[:], 1.0)
         nc.vector.tensor_copy(out=ident_bf16[:], in_=ident_f32[:])
         idle = xt_banks.tile([P, WARM, P], F32, tag="xt")
         for i in range(WARM):
             nc.tensor.matmul(idle[:, i, :], lhsT=neg_inv_count[:], rhs=neg_inv_count[:], start=True, stop=True)
+
+        nc.vector.quantize_mx(out=idle_codes[:].bitcast(FP8X4), scales=idle_plane[:], in_=idle_values[:])
 
         x_rows = x.rearrange("n h l e -> l (n h) e")
 
@@ -133,12 +140,22 @@ def tile_parallelretention_pb_s_kernel(tc, x, Wq_words, Wq_scales, bq, kv, decay
                 out=x_codes[:, n, tokens].bitcast(FP8X4), scales=x_planes[:, n, tokens], in_=grouped[:, n, values]
             )
 
-        def project(n):
-            q_t = q_banks.tile([P, L], F32, name="q_t")
+        def stir(q_t):
+            nc.tensor.matmul_mx(
+                out=q_t[:],
+                lhsT=w_words[:, 0, :].bitcast(FP4X4),
+                lhsT_scale=idle_plane[:, 0:QD],
+                rhs=idle_codes[:].bitcast(FP8X4),
+                rhs_scale=idle_plane[:],
+                start=True,
+                stop=True,
+            )
+
+        def project(n, q_t):
             for g in range(PASSES):
                 tokens = slice(g * L, (g + 1) * L)
                 nc.tensor.matmul_mx(
-                    out=q_t[:],
+                    out=q_t[:, 0:L],
                     lhsT=w_words[:, g, :].bitcast(FP4X4),
                     lhsT_scale=w_planes[:, g, :],
                     rhs=x_codes[:, n, tokens].bitcast(FP8X4),
@@ -146,12 +163,11 @@ def tile_parallelretention_pb_s_kernel(tc, x, Wq_words, Wq_scales, bq, kv, decay
                     start=(g == 0),
                     stop=(g == PASSES - 1),
                 )
-            return q_t
 
         def multiply(n, q_t):
             nc.vector.scalar_tensor_tensor(
                 out=y_t[:, n, :],
-                in0=q_t[:],
+                in0=q_t[:, 0:L],
                 scalar=bias[:, 0:1],
                 in1=g_t[:, n, :],
                 op0=ALU.add,
@@ -208,6 +224,9 @@ def tile_parallelretention_pb_s_kernel(tc, x, Wq_words, Wq_scales, bq, kv, decay
         nc.tensor.transpose(turned_2[:, 0, :], small[:, D_SLOT, :], ident_bf16[:])
         nc.scalar.copy(out=small_t[:, D_SLOT, :], in_=turned_2[:, 0, :])
         xt_0 = turn(0, BOTH)
+        q_0 = q_banks.tile([P, IDLE], F32, name="q_t")
+        stir(q_0)
+        stir(q_0)
         group(0, BOTH, xt_0)
         quantise(0, BOTH)
         xt_1 = turn(1, BOTH)
@@ -225,6 +244,7 @@ def tile_parallelretention_pb_s_kernel(tc, x, Wq_words, Wq_scales, bq, kv, decay
             )
         nc.vector.tensor_copy(out=g_t[:, 0:CUT, :], in_=g_first[:])
         xt_2 = turn(2, BOTH)
+        stir(q_0)
         group(2, BOTH, xt_2)
         nc.scalar.copy(out=g_t[:, CUT:B, :], in_=g_second[:])
         nc.tensor.transpose(turned_2[:, 1, :], small[:, BIAS_SLOT, :], ident_bf16[:])
@@ -232,22 +252,27 @@ def tile_parallelretention_pb_s_kernel(tc, x, Wq_words, Wq_scales, bq, kv, decay
 
         xt_3 = turn(3, BOTH)
         group(3, BOTH, xt_3)
-        q_0 = project(0)
+        project(0, q_0)
         quantise(1, BOTH)
         multiply(0, q_0)
         xt_4 = turn(4, BOTH)
         group(4, BOTH, xt_4)
-        q_1 = project(1)
+        q_1 = q_banks.tile([P, IDLE], F32, name="q_t")
+        stir(q_1)
+        project(1, q_1)
         quantise(2, BOTH)
         multiply(1, q_1)
         xt_5a = turn(LAST, (0,))
         group(LAST, (0,), xt_5a)
-        q_2 = project(2)
+        q_2 = q_banks.tile([P, IDLE], F32, name="q_t")
+        project(2, q_2)
         quantise(3, BOTH)
         multiply(2, q_2)
         xt_5b = turn(LAST, (1,))
         group(LAST, (1,), xt_5b)
-        q_3 = project(3)
+        q_3 = q_banks.tile([P, IDLE], F32, name="q_t")
+        stir(q_3)
+        project(3, q_3)
         quantise(4, BOTH)
         multiply(3, q_3)
 
@@ -255,12 +280,16 @@ def tile_parallelretention_pb_s_kernel(tc, x, Wq_words, Wq_scales, bq, kv, decay
         stats_0 = side_banks.tile([P, 2, WIDEST], F32, tag="side")
         sum_features(row_sum[:, 0:3], stats_0[:, 0, 0:3])
         square(0, 3, stats_0[:, 0, 0:3])
-        q_4 = project(4)
+        q_4 = q_banks.tile([P, IDLE], F32, name="q_t")
+        stir(q_4)
+        project(4, q_4)
         quantise(LAST, (0,))
         quantise(LAST, (1,))
         multiply(4, q_4)
         turn_back(0, 3, back_0)
-        q_5 = project(LAST)
+        q_5 = q_banks.tile([P, IDLE], F32, name="q_t")
+        stir(q_5)
+        project(LAST, q_5)
         multiply(LAST, q_5)
         back_1 = side_banks.tile([P, 2, QD], F32, tag="side")
         stats_1 = xt_banks.tile([P, 2, WIDEST], F32, tag="xt")

@@ -72,14 +72,14 @@ def tile_parallelretention_pb_s_kernel(tc, x, Wq_words, Wq_scales, bq, kv, decay
         ident_bf16 = keep.tile([P, P], BF16)
         neg_inv_count = keep.tile([P, P], F32)
 
+        nc.vector.memset(small[:, BIAS_SLOT, :], 0.0)
         nc.vector.memset(neg_inv_count[:], -1.0 / COUNT)
         nc.vector.memset(eps[:], EPS)
         nc.vector.memset(w_planes[:].bitcast(I32), 0)
         nc.vector.memset(ident_f32[:], 0.0)
-        nc.vector.memset(small[:, BIAS_SLOT, :], 0.0)
         nc.scalar.activation(out=table_warm[:], in_=eps[:], func=ACT.Abs_reciprocal_sqrt)
         make_identity(nc, ident_f32[:], nomemset=True)
-        nc.vector.memset(idle_values[:], 1.0)
+        nc.vector.memset(idle_values[:].bitcast(I32), 0)
         nc.vector.tensor_copy(out=ident_bf16[:], in_=ident_f32[:])
         idle = xt_banks.tile([P, WARM, P], F32, tag="xt")
         for i in range(WARM):
@@ -89,8 +89,8 @@ def tile_parallelretention_pb_s_kernel(tc, x, Wq_words, Wq_scales, bq, kv, decay
 
         x_rows = x.rearrange("n h l e -> l (n h) e")
 
-        def load_x(first, end):
-            nc.sync.dma_start(out=x_sb[:, first:end, :], in_=x_rows[:, first:end, :])
+        def load_x(n):
+            nc.sync.dma_start(out=x_sb[:, n, :], in_=x_rows[:, n, :])
 
         def load_scales(quadrant):
             nc.sync.dma_start(
@@ -102,14 +102,17 @@ def tile_parallelretention_pb_s_kernel(tc, x, Wq_words, Wq_scales, bq, kv, decay
             out=small[:, 0:B, :], in_=kv.rearrange("n h l k -> (n h l) k").rearrange("(p j) k -> p j k", j=B)
         )
         nc.sync.dma_start(out=small[:, D_SLOT, :], in_=decay_mask.rearrange("h q k -> q (h k)"))
-        load_x(0, 1)
-        nc.sync.dma_start(out=w_words[:].bitcast(I32), in_=Wq_words.rearrange("g p b -> p g b").bitcast(I32))
-        load_x(1, 3)
-        for quadrant in range(3):
-            load_scales(quadrant)
-        load_scales(3)
-        load_x(3, 5)
         nc.sync.dma_start(out=small[0:1, BIAS_SLOT, :], in_=bq.rearrange("(o q) -> o q", o=1))
+        load_x(0)
+        nc.sync.dma_start(out=w_words[:].bitcast(I32), in_=Wq_words.rearrange("g p b -> p g b").bitcast(I32))
+        load_x(1)
+        load_x(2)
+        load_scales(0)
+        load_x(3)
+        load_x(4)
+        load_scales(1)
+        load_scales(2)
+        load_scales(3)
         for g in range(PASSES):
             half = slice(g * P * PACK, (g + 1) * P * PACK)
             nc.sync.dma_start(out=x_sb[:, LAST, half], in_=x_rows[:, LAST, half])
@@ -222,13 +225,14 @@ def tile_parallelretention_pb_s_kernel(tc, x, Wq_words, Wq_scales, bq, kv, decay
         )
         turned_2 = side_banks.tile([P, 2, P], BF16, tag="side")
         nc.tensor.transpose(turned_2[:, 0, :], small[:, D_SLOT, :], ident_bf16[:])
+        nc.tensor.transpose(turned_2[:, 1, :], small[:, BIAS_SLOT, :], ident_bf16[:])
         nc.scalar.copy(out=small_t[:, D_SLOT, :], in_=turned_2[:, 0, :])
+        nc.vector.tensor_copy(out=bias[:], in_=turned_2[:, 1, 0:1])
         xt_0 = turn(0, BOTH)
-        q_0 = q_banks.tile([P, IDLE], F32, name="q_t")
-        stir(q_0)
-        stir(q_0)
         group(0, BOTH, xt_0)
         quantise(0, BOTH)
+        q_0 = q_banks.tile([P, IDLE], F32, name="q_t")
+        stir(q_0)
         xt_1 = turn(1, BOTH)
         group(1, BOTH, xt_1)
 
@@ -244,27 +248,25 @@ def tile_parallelretention_pb_s_kernel(tc, x, Wq_words, Wq_scales, bq, kv, decay
             )
         nc.vector.tensor_copy(out=g_t[:, 0:CUT, :], in_=g_first[:])
         xt_2 = turn(2, BOTH)
-        stir(q_0)
         group(2, BOTH, xt_2)
         nc.scalar.copy(out=g_t[:, CUT:B, :], in_=g_second[:])
-        nc.tensor.transpose(turned_2[:, 1, :], small[:, BIAS_SLOT, :], ident_bf16[:])
-        nc.vector.tensor_copy(out=bias[:], in_=turned_2[:, 1, 0:1])
 
         xt_3 = turn(3, BOTH)
         group(3, BOTH, xt_3)
+        stir(q_0)
         project(0, q_0)
         quantise(1, BOTH)
         multiply(0, q_0)
         xt_4 = turn(4, BOTH)
         group(4, BOTH, xt_4)
         q_1 = q_banks.tile([P, IDLE], F32, name="q_t")
-        stir(q_1)
         project(1, q_1)
         quantise(2, BOTH)
         multiply(1, q_1)
         xt_5a = turn(LAST, (0,))
         group(LAST, (0,), xt_5a)
         q_2 = q_banks.tile([P, IDLE], F32, name="q_t")
+        stir(q_2)
         project(2, q_2)
         quantise(3, BOTH)
         multiply(2, q_2)
@@ -274,6 +276,8 @@ def tile_parallelretention_pb_s_kernel(tc, x, Wq_words, Wq_scales, bq, kv, decay
         stir(q_3)
         project(3, q_3)
         quantise(4, BOTH)
+        quantise(LAST, (0,))
+        quantise(LAST, (1,))
         multiply(3, q_3)
 
         back_0 = side_banks.tile([P, 3, QD], F32, tag="side")
@@ -281,13 +285,10 @@ def tile_parallelretention_pb_s_kernel(tc, x, Wq_words, Wq_scales, bq, kv, decay
         sum_features(row_sum[:, 0:3], stats_0[:, 0, 0:3])
         square(0, 3, stats_0[:, 0, 0:3])
         q_4 = q_banks.tile([P, IDLE], F32, name="q_t")
-        stir(q_4)
         project(4, q_4)
-        quantise(LAST, (0,))
-        quantise(LAST, (1,))
         multiply(4, q_4)
         turn_back(0, 3, back_0)
-        q_5 = q_banks.tile([P, IDLE], F32, name="q_t")
+        q_5 = xt_banks.tile([P, IDLE], F32, tag="xt")
         stir(q_5)
         project(LAST, q_5)
         multiply(LAST, q_5)

@@ -249,13 +249,13 @@ def tile_parallelretention_pb_s_kernel(tc, x, Wq_words, Wq_scales, bq, kv, decay
         nc.vector.tensor_copy(out=g_t[:, 0:CUT, :], in_=g_first[:])
         xt_2 = turn(2, BOTH)
         group(2, BOTH, xt_2)
-        nc.scalar.copy(out=g_t[:, CUT:B, :], in_=g_second[:])
 
         xt_3 = turn(3, BOTH)
         group(3, BOTH, xt_3)
         stir(q_0)
         project(0, q_0)
         quantise(1, BOTH)
+        nc.vector.tensor_copy(out=g_t[:, CUT:B, :], in_=g_second[:])
         multiply(0, q_0)
         xt_4 = turn(4, BOTH)
         group(4, BOTH, xt_4)
@@ -289,7 +289,6 @@ def tile_parallelretention_pb_s_kernel(tc, x, Wq_words, Wq_scales, bq, kv, decay
         multiply(4, q_4)
         turn_back(0, 3, back_0)
         q_5 = xt_banks.tile([P, IDLE], F32, tag="xt")
-        stir(q_5)
         project(LAST, q_5)
         multiply(LAST, q_5)
         back_1 = side_banks.tile([P, 2, QD], F32, tag="side")

@@ -252,45 +252,44 @@ def tile_parallelretention_pb_s_kernel(tc, x, Wq_words, Wq_scales, bq, kv, decay
 
         xt_3 = turn(3, BOTH)
         group(3, BOTH, xt_3)
-        stir(q_0)
-        project(0, q_0)
-        quantise(1, BOTH)
-        nc.vector.tensor_copy(out=g_t[:, CUT:B, :], in_=g_second[:])
-        multiply(0, q_0)
         xt_4 = turn(4, BOTH)
         group(4, BOTH, xt_4)
-        q_1 = q_banks.tile([P, IDLE], F32, name="q_t")
-        project(1, q_1)
+        quantise(1, BOTH)
+        nc.vector.tensor_copy(out=g_t[:, CUT:B, :], in_=g_second[:])
         quantise(2, BOTH)
+        stir(q_0)
+        project(0, q_0)
+        multiply(0, q_0)
+        q_1 = q_banks.tile([P, L], F32, name="q_t")
+        project(1, q_1)
         multiply(1, q_1)
+        q_2 = side_banks.tile([P, L], F32, tag="side")
+        project(2, q_2)
+        multiply(2, q_2)
         xt_5a = turn(LAST, (0,))
         group(LAST, (0,), xt_5a)
-        q_2 = q_banks.tile([P, IDLE], F32, name="q_t")
-        stir(q_2)
-        project(2, q_2)
-        quantise(3, BOTH)
-        multiply(2, q_2)
         xt_5b = turn(LAST, (1,))
         group(LAST, (1,), xt_5b)
+        quantise(3, BOTH)
+        quantise(4, BOTH)
         q_3 = q_banks.tile([P, IDLE], F32, name="q_t")
         stir(q_3)
-        project(3, q_3)
-        quantise(4, BOTH)
-        quantise(LAST, (0,))
-        quantise(LAST, (1,))
-        multiply(3, q_3)
-
-        back_0 = side_banks.tile([P, 3, QD], F32, tag="side")
         stats_0 = side_banks.tile([P, 2, WIDEST], F32, tag="side")
         sum_features(row_sum[:, 0:3], stats_0[:, 0, 0:3])
         square(0, 3, stats_0[:, 0, 0:3])
-        q_4 = q_banks.tile([P, IDLE], F32, name="q_t")
+        project(3, q_3)
+        quantise(LAST, (0,))
+        quantise(LAST, (1,))
+        multiply(3, q_3)
+        q_4 = q_banks.tile([P, L], F32, name="q_t")
         project(4, q_4)
         multiply(4, q_4)
-        turn_back(0, 3, back_0)
-        q_5 = xt_banks.tile([P, IDLE], F32, tag="xt")
+
+        back_0 = side_banks.tile([P, 3, QD], F32, tag="side")
+        q_5 = xt_banks.tile([P, L], F32, tag="xt")
         project(LAST, q_5)
         multiply(LAST, q_5)
+        turn_back(0, 3, back_0)
         back_1 = side_banks.tile([P, 2, QD], F32, tag="side")
         stats_1 = xt_banks.tile([P, 2, WIDEST], F32, tag="xt")
         sum_features(row_sum[:, 3:5], stats_1[:, 0, 0:2])

@@ -231,8 +231,6 @@ def tile_parallelretention_pb_s_kernel(tc, x, Wq_words, Wq_scales, bq, kv, decay
         xt_0 = turn(0, BOTH)
         group(0, BOTH, xt_0)
         quantise(0, BOTH)
-        q_0 = q_banks.tile([P, IDLE], F32, name="q_t")
-        stir(q_0)
         xt_1 = turn(1, BOTH)
         group(1, BOTH, xt_1)
 
@@ -257,6 +255,7 @@ def tile_parallelretention_pb_s_kernel(tc, x, Wq_words, Wq_scales, bq, kv, decay
         quantise(1, BOTH)
         nc.vector.tensor_copy(out=g_t[:, CUT:B, :], in_=g_second[:])
         quantise(2, BOTH)
+        q_0 = q_banks.tile([P, IDLE], F32, name="q_t")
         stir(q_0)
         project(0, q_0)
         multiply(0, q_0)

from contextlib import ExitStack

import concourse.mybir as mybir
from concourse.masks import make_identity

F32 = mybir.dt.float32
BF16 = mybir.dt.bfloat16
I32 = mybir.dt.int32
U32 = mybir.dt.uint32
U8 = mybir.dt.uint8
FP8X4 = mybir.dt.float8_e4m3fn_x4
FP4X4 = mybir.dt.float4_e2m1fn_x4
ALU = mybir.AluOpType
ACT = mybir.ActivationFunctionType

P = 128
B = 6
L = 128
E = 1024
QD = 128
PACK = 4
PASSES = E // (P * PACK)
PAIRS = PACK // 2
EPS = 1e-5
COUNT = L * QD
LAST = B - 1

FLOPS = 2 * B * L * E * QD + 2 * B * L * QD * QD

WARM = 3
IDLE = 512
WIDEST = 3

D_SLOT = B
BIAS_SLOT = B + 1
SLOTS = B + 2
CUT = 4


def tile_parallelretention_pb_s_kernel(tc, x, Wq_words, Wq_scales, bq, kv, decay_mask, out):
    nc = tc.nc
    with ExitStack() as ctx:
        keep = ctx.enter_context(tc.tile_pool(name="keep", bufs=1))
        xt_banks = ctx.enter_context(tc.psum_pool(name="xt_banks", bufs=3))
        q_banks = ctx.enter_context(tc.psum_pool(name="q_banks", bufs=2))
        side_banks = ctx.enter_context(tc.psum_pool(name="side_banks", bufs=3))
        ctx.enter_context(tc.manual_schedule())

        x_sb = keep.tile([P, B, E], BF16)
        small = keep.tile([P, SLOTS, P], BF16)
        small_t = keep.tile([P, BIAS_SLOT, P], BF16)
        w_words = keep.tile([P, PASSES, 2 * QD], U8, align_bytes=64)
        w_planes = keep.tile([P, PASSES, QD], U8, align_bytes=64)
        grouped = keep.tile([P, B, PASSES * L * PACK], BF16, align_bytes=64)
        x_codes = keep.tile([P, B, PASSES * L], U32, align_bytes=64)
        x_planes = keep.tile([P, B, PASSES * L], U8, align_bytes=64)
        g_t = keep.tile([P, B, L], F32)
        y_t = keep.tile([P, B, L], F32)
        squares = keep.tile([P, B, L], F32)
        res = keep.tile([P, B, QD], F32)
        bias = keep.tile([P, 1], F32)
        row_sum = keep.tile([P, B], F32)
        row_sq = keep.tile([P, B], F32)
        neg_mean = keep.tile([P, B], F32)
        rstd = keep.tile([P, B], F32)
        eps = keep.tile([P, 1], F32)
        idle_values = keep.tile([P, IDLE * PACK], BF16, align_bytes=64)
        idle_codes = keep.tile([P, IDLE], U32, align_bytes=64)
        idle_plane = keep.tile([P, IDLE], U8, align_bytes=64)
        table_warm = keep.tile([P, 1], F32)
        ident_f32 = keep.tile([P, P], F32)
        ident_bf16 = keep.tile([P, P], BF16)
        neg_inv_count = keep.tile([P, P], F32)

        nc.vector.memset(small[:, BIAS_SLOT, :], 0.0)
        nc.vector.memset(neg_inv_count[:], -1.0 / COUNT)
        nc.vector.memset(eps[:], EPS)
        nc.vector.memset(w_planes[:].bitcast(I32), 0)
        nc.vector.memset(ident_f32[:], 0.0)
        nc.scalar.activation(out=table_warm[:], in_=eps[:], func=ACT.Abs_reciprocal_sqrt)
        make_identity(nc, ident_f32[:], nomemset=True)
        nc.vector.memset(idle_values[:].bitcast(I32), 0)
        nc.vector.tensor_copy(out=ident_bf16[:], in_=ident_f32[:])
        idle = xt_banks.tile([P, WARM, P], F32, tag="xt")
        for i in range(WARM):
            nc.tensor.matmul(idle[:, i, :], lhsT=neg_inv_count[:], rhs=neg_inv_count[:], start=True, stop=True)

        nc.vector.quantize_mx(out=idle_codes[:].bitcast(FP8X4), scales=idle_plane[:], in_=idle_values[:])

        x_rows = x.rearrange("n h l e -> l (n h) e")

        def load_x(n):
            nc.sync.dma_start(out=x_sb[:, n, :], in_=x_rows[:, n, :])

        def load_scales(quadrant):
            nc.sync.dma_start(
                out=w_planes[28 * quadrant : 28 * quadrant + 16, :, :].bitcast(I32),
                in_=Wq_scales.rearrange("g r q -> r g q").bitcast(I32),
            )

        nc.sync.dma_start(
            out=small[:, 0:B, :], in_=kv.rearrange("n h l k -> (n h l) k").rearrange("(p j) k -> p j k", j=B)
        )
        nc.sync.dma_start(out=small[:, D_SLOT, :], in_=decay_mask.rearrange("h q k -> q (h k)"))
        nc.sync.dma_start(out=small[0:1, BIAS_SLOT, :], in_=bq.rearrange("(o q) -> o q", o=1))
        load_x(0)
        nc.sync.dma_start(out=w_words[:].bitcast(I32), in_=Wq_words.rearrange("g p b -> p g b").bitcast(I32))
        load_x(1)
        load_x(2)
        load_scales(0)
        load_x(3)
        load_x(4)
        load_scales(1)
        load_scales(2)
        load_scales(3)
        for g in range(PASSES):
            half = slice(g * P * PACK, (g + 1) * P * PACK)
            nc.sync.dma_start(out=x_sb[:, LAST, half], in_=x_rows[:, LAST, half])

        WORDS = P * PAIRS

        def turn(n, passes):
            xt = xt_banks.tile([P, len(passes), PAIRS, L], F32, name="xt")
            x_words = x_sb[:, n, :].bitcast(F32)
            for i, g in enumerate(passes):
                for u in range(PAIRS):
                    nc.tensor.transpose(
                        xt[:, i, u, :], x_words[:, WORDS * g + u : WORDS * (g + 1) : PAIRS], ident_f32[:]
                    )
            return xt

        def group(n, passes, xt):
            values = slice(passes[0] * L * PACK, (passes[-1] + 1) * L * PACK)
            nc.scalar.copy(
                out=grouped[:, n, values].bitcast(F32).rearrange("p (g l u) -> p g l u", l=L, u=PAIRS),
                in_=xt[:].rearrange("p g u l -> p g l u"),
            )

        def quantise(n, passes):
            values = slice(passes[0] * L * PACK, (passes[-1] + 1) * L * PACK)
            tokens = slice(passes[0] * L, (passes[-1] + 1) * L)
            nc.vector.quantize_mx(
                out=x_codes[:, n, tokens].bitcast(FP8X4), scales=x_planes[:, n, tokens], in_=grouped[:, n, values]
            )

        def stir(q_t):
            nc.tensor.matmul_mx(
                out=q_t[:],
                lhsT=w_words[:, 0, :].bitcast(FP4X4),
                lhsT_scale=idle_plane[:, 0:QD],
                rhs=idle_codes[:].bitcast(FP8X4),
                rhs_scale=idle_plane[:],
                start=True,
                stop=True,
            )

        def project(n, q_t):
            for g in range(PASSES):
                tokens = slice(g * L, (g + 1) * L)
                nc.tensor.matmul_mx(
                    out=q_t[:, 0:L],
                    lhsT=w_words[:, g, :].bitcast(FP4X4),
                    lhsT_scale=w_planes[:, g, :],
                    rhs=x_codes[:, n, tokens].bitcast(FP8X4),
                    rhs_scale=x_planes[:, n, tokens],
                    start=(g == 0),
                    stop=(g == PASSES - 1),
                )

        def multiply(n, q_t):
            nc.vector.scalar_tensor_tensor(
                out=y_t[:, n, :],
                in0=q_t[:, 0:L],
                scalar=bias[:, 0:1],
                in1=g_t[:, n, :],
                op0=ALU.add,
                op1=ALU.mult,
                accum_out=row_sum[:, n : n + 1],
            )

        def sum_features(columns, stats):
            nc.tensor.matmul(stats, lhsT=neg_inv_count[:], rhs=columns, start=True, stop=True)

        def turn_back(first, end, back):
            for n in range(first, end):
                nc.tensor.transpose(back[:, n - first, :], y_t[:, n, :], ident_f32[:])

        def square(first, end, stats):
            nc.scalar.copy(out=neg_mean[:, first:end], in_=stats)
            for n in range(first, end):
                nc.scalar.activation(
                    out=squares[:, n, :],
                    in_=y_t[:, n, :],
                    func=ACT.Square,
                    bias=neg_mean[:, n : n + 1],
                    scale=1.0,
                    accum_out=row_sq[:, n : n + 1],
                )

        def deviation(first, end, stats):
            nc.scalar.activation(
                out=rstd[:, first:end], in_=stats, func=ACT.Abs_reciprocal_sqrt, bias=eps[:, 0:1], scale=-1.0
            )

        def normalise(first, end, back):
            for n in range(first, end):
                nc.vector.tensor_scalar(
                    out=res[:, n, :],
                    in0=back[:, n - first, :],
                    scalar1=neg_mean[:, n : n + 1],
                    scalar2=rstd[:, n : n + 1],
                    op0=ALU.add,
                    op1=ALU.mult,
                )
            nc.sync.dma_start(out=out[first:end].rearrange("n l q -> l n q"), in_=res[:, first:end, :])

        BOTH = (0, 1)

        turned = side_banks.tile([P, B, P], BF16, tag="side")
        for j in range(B):
            nc.tensor.transpose(turned[:, j, :], small[:, j, :], ident_bf16[:])
        nc.vector.tensor_copy(
            out=small_t[:, 0:B, :].rearrange("k n l -> k (n l)").rearrange("k (p j) -> k p j", j=B),
            in_=turned[:].rearrange("k j p -> k p j"),
        )
        turned_2 = side_banks.tile([P, 2, P], BF16, tag="side")
        nc.tensor.transpose(turned_2[:, 0, :], small[:, D_SLOT, :], ident_bf16[:])
        nc.tensor.transpose(turned_2[:, 1, :], small[:, BIAS_SLOT, :], ident_bf16[:])
        nc.scalar.copy(out=small_t[:, D_SLOT, :], in_=turned_2[:, 0, :])
        nc.vector.tensor_copy(out=bias[:], in_=turned_2[:, 1, 0:1])
        xt_0 = turn(0, BOTH)
        group(0, BOTH, xt_0)
        quantise(0, BOTH)
        xt_1 = turn(1, BOTH)
        group(1, BOTH, xt_1)

        g_first = side_banks.tile([P, CUT, L], F32, tag="side")
        g_second = side_banks.tile([P, B - CUT, L], F32, tag="side")
        for bank, first, end in ((g_first, 0, CUT), (g_second, CUT, B)):
            nc.tensor.matmul(
                bank[:].rearrange("q n l -> q (n l)"),
                lhsT=small_t[:, D_SLOT, :],
                rhs=small_t[:, first:end, :].rearrange("k n l -> k (n l)"),
                start=True,
                stop=True,
            )
        nc.vector.tensor_copy(out=g_t[:, 0:CUT, :], in_=g_first[:])
        xt_2 = turn(2, BOTH)
        group(2, BOTH, xt_2)

        xt_3 = turn(3, BOTH)
        group(3, BOTH, xt_3)
        xt_4 = turn(4, BOTH)
        group(4, BOTH, xt_4)
        quantise(1, BOTH)
        nc.vector.tensor_copy(out=g_t[:, CUT:B, :], in_=g_second[:])
        quantise(2, BOTH)
        q_0 = q_banks.tile([P, IDLE], F32, name="q_t")
        stir(q_0)
        project(0, q_0)
        multiply(0, q_0)
        q_1 = q_banks.tile([P, L], F32, name="q_t")
        project(1, q_1)
        multiply(1, q_1)
        q_2 = side_banks.tile([P, L], F32, tag="side")
        project(2, q_2)
        multiply(2, q_2)
        xt_5a = turn(LAST, (0,))
        group(LAST, (0,), xt_5a)
        xt_5b = turn(LAST, (1,))
        group(LAST, (1,), xt_5b)
        quantise(3, BOTH)
        quantise(4, BOTH)
        q_3 = q_banks.tile([P, IDLE], F32, name="q_t")
        stir(q_3)
        stats_0 = side_banks.tile([P, 2, WIDEST], F32, tag="side")
        sum_features(row_sum[:, 0:3], stats_0[:, 0, 0:3])
        square(0, 3, stats_0[:, 0, 0:3])
        project(3, q_3)
        quantise(LAST, (0,))
        quantise(LAST, (1,))
        multiply(3, q_3)
        q_4 = q_banks.tile([P, L], F32, name="q_t")
        project(4, q_4)
        multiply(4, q_4)

        back_0 = side_banks.tile([P, 3, QD], F32, tag="side")
        q_5 = xt_banks.tile([P, L], F32, tag="xt")
        project(LAST, q_5)
        multiply(LAST, q_5)
        turn_back(0, 3, back_0)
        back_1 = side_banks.tile([P, 2, QD], F32, tag="side")
        stats_1 = xt_banks.tile([P, 2, WIDEST], F32, tag="xt")
        sum_features(row_sum[:, 3:5], stats_1[:, 0, 0:2])
        square(3, 5, stats_1[:, 0, 0:2])
        sum_features(row_sq[:, 0:3], stats_0[:, 1, 0:3])
        deviation(0, 3, stats_0[:, 1, 0:3])
        normalise(0, 3, back_0)
        back_2 = xt_banks.tile([P, 1, QD], F32, tag="xt")
        stats_2 = xt_banks.tile([P, 2, WIDEST], F32, tag="xt")
        sum_features(row_sum[:, 5:6], stats_2[:, 0, 0:1])
        square(5, 6, stats_2[:, 0, 0:1])
        turn_back(3, 5, back_1)
        turn_back(5, 6, back_2)
        sum_features(row_sq[:, 3:5], stats_1[:, 1, 0:2])
        deviation(3, 5, stats_1[:, 1, 0:2])
        normalise(3, 5, back_1)
        sum_features(row_sq[:, 5:6], stats_2[:, 1, 0:1])
        deviation(5, 6, stats_2[:, 1, 0:1])
        normalise(5, 6, back_2)
